import numpy as np
import ml_dtypes


def mxq(x, axis, fmt="e4m3"):
    dtype, down = {"e4m3": (ml_dtypes.float8_e4m3fn, 7), "e5m2": (ml_dtypes.float8_e5m2, 14)}[fmt]
    v = np.moveaxis(np.asarray(x, np.float32).astype(ml_dtypes.bfloat16).astype(np.float64), axis, -1)
    blocks = v.reshape(v.shape[:-1] + (-1, 32))
    amax = np.abs(blocks).max(-1, keepdims=True)
    byte = np.maximum(np.where(amax > 0, np.frexp(amax)[1] - 1 + 127, 0) - down, 1)
    scale = np.exp2(byte - 127.0)
    codes = (blocks / scale).astype(np.float32).astype(dtype).astype(np.float64)
    return np.moveaxis((codes * scale).reshape(v.shape), -1, axis)


WIDE = False


def mx_kscale(k):
    if not WIDE:
        return np.ones(k)
    levels = np.array([10, -10, 5, -5, 0])
    a = np.random.permutation(np.resize(levels, k // 512 * 4)).reshape(k // 512, 4)
    idx = np.arange(k)
    return np.exp2(a[idx // 512, idx % 128 // 32])


BF16 = ml_dtypes.bfloat16


def bf(x):
    return np.asarray(x, np.float32).astype(BF16)


def f64(x):
    return np.asarray(x).astype(np.float64)


E2M1 = np.array([0.0, 0.5, 1.0, 1.5, 2.0, 3.0, 4.0, 6.0, -0.0, -0.5, -1.0, -1.5, -2.0, -3.0, -4.0, -6.0])


def pack_weight(w, fmt):
    k, n = w.shape
    w = f64(bf(w)).reshape(k // 32, 32, n)
    amax = np.abs(w).max(1)
    if fmt == "e4m3":
        byte = np.frexp(amax)[1] - 1 + 127 - 7
    else:
        mant, ex = np.frexp(amax / 6.0)
        byte = np.where(mant > 0.5, ex, ex - 1) + 127
    byte = np.clip(np.where(amax > 0, byte, 1), 1, 254)
    scaled = (w * np.exp2(127.0 - byte)[:, None, :]).reshape(k, n).astype(np.float32)
    by_word = np.ascontiguousarray(scaled.reshape(k // 512, 128, 4, n).transpose(0, 1, 3, 2))
    if fmt == "e4m3":
        words = by_word.astype(ml_dtypes.float8_e4m3fn).view(np.uint8)
    else:
        c = by_word.astype(ml_dtypes.float4_e2m1fn).view(np.uint8) & 0xF
        words = c[..., 0::2] | (c[..., 1::2] << 4)
    return np.ascontiguousarray(words), np.ascontiguousarray(byte.astype(np.uint8).reshape(k // 512, 16, n))


def unpack_weight(words, scales, fmt):
    g, p, n, _ = words.shape
    if fmt == "e4m3":
        vals = np.ascontiguousarray(words).view(ml_dtypes.float8_e4m3fn).astype(np.float64)
    else:
        nib = np.empty((g, p, n, 4), np.uint8)
        nib[..., 0::2] = words & 0xF
        nib[..., 1::2] = words >> 4
        vals = E2M1[nib]
    vals = vals * np.repeat(np.exp2(scales.astype(np.float64) - 127.0), 8, axis=1)[..., None]
    return vals.transpose(0, 1, 3, 2).reshape(g * 512, n)


B, F_IN, HID, E, G, H = 4096, 64, 1024, 32, 4, 8
BN_EPS = 1e-5
L1_EPS = 1e-6 ** 2
SELU_ALPHA = 1.6732632423543772
SELU_SCALE = 1.0507009873554805


def selu(v):
    return SELU_SCALE * np.where(v > 0.0, v, SELU_ALPHA * (np.exp(np.minimum(v, 0.0)) - 1.0))


def setup_inputs():
    s = mx_kscale(HID)
    t = s / s.min()
    col_std = 0.5 + np.random.random(HID)
    col_mean = 0.5 * np.random.standard_normal(HID)
    h2 = bf(np.random.standard_normal((B, HID)) * col_std + col_mean)
    gamma = bf((1.0 + 0.1 * np.random.standard_normal(HID)) * t)
    beta = bf(0.1 * np.random.standard_normal(HID) * t)
    stack = np.random.standard_normal((H, G, HID, E)) / np.sqrt(HID) / t[:, None]
    words, scales = pack_weight(stack.reshape(-1, E), "e4m3")
    bh = bf(0.3 * np.random.standard_normal((H, G, E)))
    return {"h2": h2,
            "gamma": gamma,
            "beta": beta,
            "Wh_words": words,
            "Wh_scales": scales,
            "bh": bh}


def reference(h2, gamma, beta, Wh_words, Wh_scales, bh):
    h2 = f64(h2)
    mu = h2.mean(axis=0)
    var = h2.var(axis=0)
    e = selu((h2 - mu) / np.sqrt(var + BN_EPS) * f64(gamma) + f64(beta))
    p = (mxq(e, 1, "e4m3") @ unpack_weight(Wh_words, Wh_scales, "e4m3").reshape(H, G, HID, E)).transpose(2, 0, 1, 3)
    d = selu(p + f64(bh))
    a = np.abs(d)
    l1 = np.maximum(a.sum(axis=-1, keepdims=True), L1_EPS)
    return np.sign(d) * (a / l1)

@@ -1,0 +1,371 @@
+import math
+from contextlib import ExitStack
+
+import concourse.mybir as mybir
+from concourse.masks import make_identity
+
+F32 = mybir.dt.float32
+BF16 = mybir.dt.bfloat16
+I32 = mybir.dt.int32
+U32 = mybir.dt.uint32
+U8 = mybir.dt.uint8
+FP8X4 = mybir.dt.float8_e4m3fn_x4
+ACT = mybir.ActivationFunctionType
+ALU = mybir.AluOpType
+AXIS = mybir.AxisListType
+
+P = 128
+ROWS = 4096
+FEATURES = 1024
+OUTPUTS = 1024
+HEAD = 32
+PACK = 4
+K_PASS = P * PACK
+PASSES = FEATURES // K_PASS
+BLOCK = 512
+SUBS = BLOCK // P
+N_BLOCKS = ROWS // BLOCK
+OUT_TILES = OUTPUTS // P
+HALF_TILES = OUT_TILES // 2
+HEADS = OUTPUTS // HEAD
+E_LOW = HEAD // OUT_TILES
+AHEAD = 2
+VECTOR_RELU_TILES = (0, 1, 2)
+STAT_CHUNK = 512
+
+BN_EPS = 1e-5
+L1_EPS = 1e-12
+SELU_ALPHA = 1.6732632423543772
+SELU_SCALE = 1.0507009873554805
+SCALE_ALPHA = SELU_SCALE * SELU_ALPHA
+
+FLOPS = 2 * ROWS * FEATURES * OUTPUTS
+
+
+def tile_basicemotionpredictions_pa_t_e_kernel(tc, h2, gamma, beta, Wh_words, Wh_scales, bh, out):
+    nc = tc.nc
+    out_rows = out.rearrange("b h g e -> b (h g e)")
+
+    with ExitStack() as ctx:
+        const = ctx.enter_context(tc.tile_pool(name="const", bufs=1))
+        xpool = ctx.enter_context(tc.tile_pool(name="x", bufs=1))
+        act1 = ctx.enter_context(tc.tile_pool(name="act1", bufs=2))
+        quant = ctx.enter_context(tc.tile_pool(name="quant", bufs=4))
+        act2 = ctx.enter_context(tc.tile_pool(name="act2", bufs=3))
+        dpool = ctx.enter_context(tc.tile_pool(name="d", bufs=OUT_TILES))
+        wpool = ctx.enter_context(tc.tile_pool(name="w", bufs=6))
+        opool = ctx.enter_context(tc.tile_pool(name="o", bufs=3))
+        small = ctx.enter_context(tc.tile_pool(name="small", bufs=2))
+        scrap = ctx.enter_context(tc.tile_pool(name="scrap", bufs=4))
+        xt_psum = ctx.enter_context(tc.psum_pool(name="xt_psum", bufs=2))
+        pm_psum = ctx.enter_context(tc.psum_pool(name="pm_psum", bufs=3))
+        tv_psum = ctx.enter_context(tc.psum_pool(name="tv_psum", bufs=3))
+
+        x_blocks = []
+
+        def load_x(blk):
+            x_blk = xpool.tile([P, SUBS, FEATURES], BF16, name="x%d" % blk)
+            nc.sync.dma_start(
+                out=x_blk[:],
+                in_=h2[blk * BLOCK : (blk + 1) * BLOCK, :].rearrange("(p s) k -> p s k", s=SUBS),
+            )
+            x_blocks.append(x_blk)
+
+        for blk in range(N_BLOCKS):
+            load_x(blk)
+
+        gamma_bf = const.tile([P, PASSES, PACK], BF16)
+        beta_bf = const.tile([P, PASSES, PACK], BF16)
+        nc.scalar.dma_start(out=gamma_bf[:], in_=gamma.rearrange("(c p t) -> p c t", c=PASSES, t=PACK))
+        nc.scalar.dma_start(out=beta_bf[:], in_=beta.rearrange("(c p t) -> p c t", c=PASSES, t=PACK))
+        bh_bf = const.tile([P, OUT_TILES], BF16)
+        bh_heads = bh.rearrange("h g e -> (h g) e")
+        with nc.allow_non_contiguous_dma(reason="1,024 bias values, one to a partition and column"):
+            for e in range(E_LOW):
+                nc.scalar.dma_start(out=bh_bf[e:P:E_LOW, :], in_=bh_heads[:, e:HEAD:E_LOW])
+
+        ident = const.tile([P, P], F32)
+        make_identity(nc, ident[:])
+
+        w_raw = act1.tile([P, PASSES, OUTPUTS], I32, name="w_raw", tag="lin")
+        planes_raw = act1.tile([P, PASSES, OUTPUTS // 4], I32, name="planes_raw", tag="neg")
+        w_words = const.tile([P, PASSES, OUTPUTS], U32, align_bytes=64)
+        w_planes = const.tile([P, PASSES, OUTPUTS], U8, align_bytes=64)
+        nc.vector.memset(planes_raw[:].rearrange("p c n -> p (c n)"), 0)
+        words_dram = Wh_words.rearrange("g p n t -> g p (n t)").bitcast(I32).rearrange("(m c) p n -> c p m n", c=PASSES)
+        scales_dram = Wh_scales.bitcast(I32).rearrange("(m c) q w -> c q m w", c=PASSES)
+        for c in range(PASSES):
+            nc.sync.dma_start(out=w_raw[:, c, :].rearrange("p (m n) -> p m n", n=HEAD), in_=words_dram[c])
+        for c in range(PASSES):
+            for quad in range(4):
+                nc.sync.dma_start(
+                    out=planes_raw[32 * quad : 32 * quad + 4, c, :].rearrange("r (m w) -> r m w", w=HEAD // 4),
+                    in_=scales_dram[c, 4 * quad : 4 * quad + 4],
+                )
+        for c in range(PASSES):
+            nc.gpsimd.tensor_copy(
+                out=w_words[:, c, :].bitcast(I32).rearrange("p (j m e) -> p j m e", j=OUT_TILES, e=E_LOW),
+                in_=w_raw[:, c, :].rearrange("p (m j e) -> p j m e", j=OUT_TILES, e=E_LOW),
+            )
+            nc.gpsimd.tensor_copy(
+                out=w_planes[:, c, :].bitcast(I32).rearrange("p (j m) -> p j m", j=OUT_TILES),
+                in_=planes_raw[:, c, :].rearrange("p (m j) -> p j m", j=OUT_TILES),
+            )
+
+        warm_in = const.tile([P, 1], F32)
+        warm_sqrt = const.tile([P, 1], F32)
+        warm_exp = const.tile([P, 1], F32)
+        nc.vector.memset(warm_in[:], 1.0)
+        nc.scalar.activation(out=warm_sqrt[:], in_=warm_in[:], func=ACT.Sqrt)
+
+        def transpose_features(blk, c, u, pool, tag):
+            x_words = x_blocks[blk][:].bitcast(F32)
+            xt = pool.tile([P, BLOCK], F32, name="xt", tag=tag)
+            for s in range(SUBS):
+                nc.tensor.transpose(
+                    out=xt[:, s * P : (s + 1) * P],
+                    in_=x_words[:, s, 256 * c + u : 256 * (c + 1) : 2],
+                    identity=ident[:],
+                )
+            return xt
+
+        chunks = N_BLOCKS * 2 * BLOCK // STAT_CHUNK
+        vector_banks = 2 * PASSES - 1
+        n_feat = PASSES * PACK
+        stats = const.tile([P, vector_banks, chunks, 6], F32)
+        neg_pivot = const.tile([P, 2], F32)
+        sums = const.tile([P, 2, 2, N_BLOCKS], F32)
+        for blk in range(N_BLOCKS):
+            for c in range(PASSES):
+                for u in range(2):
+                    if 2 * c + u < vector_banks:
+                        xt = transpose_features(blk, c, u, xt_psum, "xt")
+                    else:
+                        xt = transpose_features(blk, c, u, tv_psum, "values")
+                    pairs = xt[:].bitcast(BF16)
+                    if 2 * c + u < vector_banks:
+                        for h in range(2):
+                            nc.vector.bn_stats(
+                                out=stats[:, 2 * c + u, 2 * blk + h, :],
+                                in_=pairs[:, h * STAT_CHUNK : (h + 1) * STAT_CHUNK],
+                            )
+                    else:
+                        if blk == 0:
+                            nc.vector.tensor_scalar_mul(out=neg_pivot[:], in0=pairs[:, 0:2], scalar1=-1.0)
+                        by_feature = pairs.rearrange("p (b e) -> p b e", e=2)
+                        for e in range(2):
+                            centred = scrap.tile([P, BLOCK], BF16, name="centred")
+                            squared = scrap.tile([P, BLOCK], BF16, name="squared")
+                            nc.scalar.activation(
+                                out=centred[:], in_=by_feature[:, :, e], func=ACT.Identity,
+                                bias=neg_pivot[:, e : e + 1], scale=1.0, accum_out=sums[:, e, 0, blk : blk + 1],
+                            )
+                            nc.scalar.activation(
+                                out=squared[:], in_=by_feature[:, :, e], func=ACT.Square,
+                                bias=neg_pivot[:, e : e + 1], scale=1.0, accum_out=sums[:, e, 1, blk : blk + 1],
+                            )
+        mean_var = const.tile([P, n_feat, 2], F32)
+        for cu in range(vector_banks):
+            for e in range(2):
+                nc.vector.bn_aggr(out=mean_var[:, 2 * cu + e, :], in_=stats[:, cu, :, 3 * e : 3 * e + 3])
+        moments = const.tile([P, 2, 2], F32)
+        m1_squared = const.tile([P, 2], F32)
+        nc.vector.tensor_reduce(out=moments[:], in_=sums[:], axis=AXIS.X, op=ALU.add)
+        nc.vector.tensor_scalar_mul(out=moments[:], in0=moments[:], scalar1=1.0 / ROWS)
+        nc.vector.tensor_sub(out=mean_var[:, 2 * vector_banks :, 0], in0=moments[:, :, 0], in1=neg_pivot[:])
+        nc.vector.tensor_mul(out=m1_squared[:], in0=moments[:, :, 0], in1=moments[:, :, 0])
+        nc.vector.tensor_sub(out=mean_var[:, 2 * vector_banks :, 1], in0=moments[:, :, 1], in1=m1_squared[:])
+
+        var_eps = const.tile([P, n_feat], F32)
+        std = const.tile([P, n_feat], F32)
+        rstd = const.tile([P, n_feat], F32)
+        gain = const.tile([P, n_feat], F32)
+        mean_gain = const.tile([P, n_feat], F32)
+        shift = const.tile([P, n_feat], F32)
+        lin_scale = const.tile([P, n_feat], F32)
+        lin_bias = const.tile([P, n_feat], F32)
+        zero = const.tile([P, 1], F32)
+        exp1_bias = const.tile([P, 1], F32)
+        nc.vector.tensor_scalar_add(out=var_eps[:], in0=mean_var[:, :, 1], scalar1=BN_EPS)
+        nc.scalar.activation(out=std[:], in_=var_eps[:], func=ACT.Sqrt)
+        nc.scalar.activation(out=warm_exp[:], in_=std[:, 0:1], func=ACT.Exp)
+        nc.vector.reciprocal(out=rstd[:], in_=std[:])
+        nc.vector.tensor_mul(out=gain[:], in0=rstd[:], in1=gamma_bf[:].rearrange("p c t -> p (c t)"))
+        nc.vector.tensor_mul(out=mean_gain[:], in0=mean_var[:, :, 0], in1=gain[:])
+        nc.vector.tensor_sub(out=shift[:], in0=beta_bf[:].rearrange("p c t -> p (c t)"), in1=mean_gain[:])
+        nc.vector.tensor_scalar_mul(out=lin_scale[:], in0=gain[:], scalar1=SELU_SCALE)
+        nc.vector.tensor_scalar(
+            out=lin_bias[:], in0=shift[:], scalar1=SELU_SCALE, scalar2=-SCALE_ALPHA, op0=ALU.mult, op1=ALU.add,
+        )
+        nc.vector.memset(zero[:], 0.0)
+        nc.vector.tensor_scalar_add(out=exp1_bias[:], in0=zero[:], scalar1=SELU_ALPHA + math.log(SCALE_ALPHA))
+
+        relu2_bias = const.tile([P, OUT_TILES], F32)
+        exp2_bias = const.tile([P, OUT_TILES], F32)
+        nc.vector.tensor_copy(out=relu2_bias[:], in_=bh_bf[:])
+        nc.vector.tensor_scalar_add(out=exp2_bias[:], in0=bh_bf[:], scalar1=math.log(SELU_ALPHA))
+
+        branches = {}
+        clamped = {}
+        exps = {}
+        joined = {}
+        e_mx = {}
+        pairs = {}
+        sums2 = {}
+        invs = {}
+        outs = {}
+
+        def linear_branch(blk, c, u):
+            if u == 0:
+                lin = act1.tile([P, PACK, BLOCK], F32, name="lin")
+                branches[(blk, c)] = lin
+            lin = branches[(blk, c)]
+            xt = transpose_features(blk, c, u, xt_psum, "xt")
+            pairs = xt[:].bitcast(BF16).rearrange("p (b e) -> p b e", e=2)
+            for e in range(2):
+                t = 2 * u + e
+                f = PACK * c + t
+                nc.scalar.activation(
+                    out=lin[:, t, :], in_=pairs[:, :, e], func=ACT.Identity,
+                    bias=lin_bias[:, f : f + 1], scale=lin_scale[:, f : f + 1],
+                )
+
+        def clamp(blk, c):
+            neg = act1.tile([P, PACK, BLOCK], F32, name="neg")
+            nc.vector.tensor_scalar_min(out=neg[:], in0=branches[(blk, c)][:], scalar1=-SCALE_ALPHA)
+            clamped[(blk, c)] = neg
+
+        def exp_branch(blk, c):
+            expo = clamped[(blk, c)]
+            nc.scalar.activation(
+                out=expo[:], in_=expo[:], func=ACT.Exp, bias=exp1_bias[:, 0:1], scale=1.0 / SELU_SCALE,
+            )
+            exps[(blk, c)] = expo
+
+        def join_e(blk, c):
+            grouped = act1.tile([P, BLOCK, PACK], BF16, name="grouped", align_bytes=64)
+            joined[(blk, c)] = grouped
+            nc.vector.scalar_tensor_tensor(
+                out=grouped[:],
+                in0=branches[(blk, c)][:].rearrange("p t b -> p b t"),
+                scalar=-SCALE_ALPHA,
+                in1=exps[(blk, c)][:].rearrange("p t b -> p b t"),
+                op0=ALU.max,
+                op1=ALU.add,
+            )
+
+        def quantise_e(blk, c):
+            grouped = joined[(blk, c)]
+            e_words = quant.tile([P, BLOCK], U32, name="e_words", align_bytes=64)
+            e_plane = quant.tile([P, BLOCK], U8, name="e_plane", align_bytes=64)
+            nc.vector.quantize_mx(
+                out=e_words[:].bitcast(FP8X4),
+                scales=e_plane[:],
+                in_=grouped[:].rearrange("p b t -> p (b t)"),
+            )
+            e_mx[(blk, c)] = (e_words, e_plane)
+
+        def heads(blk, j):
+            cols = slice(j * P, (j + 1) * P)
+            pm = pm_psum.tile([P, BLOCK], F32, name="pm")
+            for c in range(PASSES):
+                e_words, e_plane = e_mx[(blk, c)]
+                nc.tensor.matmul_mx(
+                    out=pm[:],
+                    lhsT=w_words[:, c, cols].bitcast(FP8X4),
+                    lhsT_scale=w_planes[:, c, cols],
+                    rhs=e_words[:].bitcast(FP8X4),
+                    rhs_scale=e_plane[:],
+                    start=(c == 0),
+                    stop=(c == PASSES - 1),
+                )
+            if j % 2 == 0:
+                d_pair = dpool.tile([P, 2, BLOCK], F32, name="d_pair")
+                w_pair = wpool.tile([P, 2, BLOCK], F32, name="w_pair")
+                pairs[(blk, j // 2)] = (d_pair, w_pair)
+            d_pair, w_pair = pairs[(blk, j // 2)]
+            exp2 = act2.tile([P, BLOCK], F32, name="exp2")
+            pos = act2.tile([P, BLOCK], F32, name="pos")
+            nc.scalar.activation(out=exp2[:], in_=pm[:], func=ACT.Exp, bias=exp2_bias[:, j : j + 1], scale=1.0)
+            if j in VECTOR_RELU_TILES:
+                nc.vector.tensor_scalar(
+                    out=pos[:], in0=pm[:], scalar1=relu2_bias[:, j : j + 1], scalar2=0.0, op0=ALU.add, op1=ALU.max,
+                )
+            else:
+                nc.scalar.activation(out=pos[:], in_=pm[:], func=ACT.Relu, bias=relu2_bias[:, j : j + 1], scale=1.0)
+            nc.vector.scalar_tensor_tensor(
+                out=d_pair[:, j % 2, :], in0=exp2[:], scalar=-SELU_ALPHA, in1=pos[:], op0=ALU.add, op1=ALU.min,
+            )
+            if j % 2 == 1:
+                nc.scalar.activation(out=w_pair[:], in_=d_pair[:], func=ACT.Abs)
+
+        def turned(dest, blk, j, which, s, start, stop):
+            nc.tensor.matmul(
+                out=dest,
+                lhsT=pairs[(blk, j // 2)][which][:, j % 2, s * P : (s + 1) * P],
+                rhs=ident[:],
+                is_transpose=True,
+                start=start,
+                stop=stop,
+            )
+
+        def norm_sums(blk, s):
+            if s == 0:
+                sums2[blk] = tv_psum.tile([P, SUBS, P], F32, name="sum_w", tag="values")
+            for j in range(OUT_TILES):
+                turned(sums2[blk][:, s, :], blk, j, 1, s, j == 0, j == OUT_TILES - 1)
+
+        def norm_finish(blk):
+            l1 = small.tile([P, SUBS * HEADS], F32, name="l1")
+            l1_floor = small.tile([P, SUBS * HEADS], F32, name="l1_floor")
+            inv = small.tile([P, SUBS, HEADS], F32, name="inv")
+            nc.vector.tensor_reduce(
+                out=l1[:], in_=sums2[blk][:].rearrange("p s (m e) -> p (s m) e", e=E_LOW), axis=AXIS.X, op=ALU.add,
+            )
+            nc.vector.tensor_scalar_max(out=l1_floor[:], in0=l1[:], scalar1=L1_EPS / SELU_SCALE)
+            nc.vector.reciprocal(out=inv[:].rearrange("p s m -> p (s m)"), in_=l1_floor[:])
+            invs[blk] = inv
+
+        def normalise_and_store(blk, s, half):
+            rows = out_rows[blk * BLOCK : (blk + 1) * BLOCK, :].rearrange("(p s) n -> p s n", s=SUBS)
+            values = tv_psum.tile([P, HEADS, HALF_TILES * E_LOW], F32, name="values")
+            for jj in range(HALF_TILES):
+                turned(values[:, :, jj * E_LOW : (jj + 1) * E_LOW], blk, half * HALF_TILES + jj, 0, s, True, True)
+            if half == 0:
+                o = opool.tile([P, HEADS, HEAD], F32, name="o")
+                outs[(blk, s)] = o
+            o = outs[(blk, s)]
+            span = HALF_TILES * E_LOW
+            nc.vector.tensor_tensor(
+                out=o[:, :, half * span : (half + 1) * span],
+                in0=values[:],
+                in1=invs[blk][:, s, :].unsqueeze(2).to_broadcast([P, HEADS, span]),
+                op=ALU.mult,
+            )
+            if half == 1:
+                nc.sync.dma_start(out=rows[:, s, :], in_=o[:].rearrange("p m e -> p (m e)"))
+
+        for step in range(-OUT_TILES - AHEAD, OUT_TILES * (N_BLOCKS + 1)):
+            blk, j = divmod(step, OUT_TILES)
+            nxt, je = divmod(step + OUT_TILES + AHEAD, OUT_TILES)
+            prev = blk - 1
+            qb, qe = divmod(step - 1 + OUT_TILES + AHEAD, OUT_TILES)
+            if je % 4 < 2 and nxt < N_BLOCKS:
+                linear_branch(nxt, je // 4, je % 4)
+            if je % 4 == 1 and nxt < N_BLOCKS:
+                clamp(nxt, je // 4)
+            if je % 4 == 2 and nxt < N_BLOCKS:
+                exp_branch(nxt, je // 4)
+            if 0 <= blk < N_BLOCKS:
+                heads(blk, j)
+            if qe % 4 == 3 and 0 <= qb < N_BLOCKS:
+                quantise_e(qb, qe // 4)
+            if je % 4 == 3 and nxt < N_BLOCKS:
+                join_e(nxt, je // 4)
+            if prev >= 0 and j < SUBS:
+                norm_sums(prev, j)
+            if prev >= 0 and j == SUBS - 1:
+                norm_finish(prev)
+            if prev >= 0 and j >= SUBS:
+                normalise_and_store(prev, j - SUBS, 0)
+                normalise_and_store(prev, j - SUBS, 1)

@@ -30,9 +30,15 @@ HALF_TILES = OUT_TILES // 2
 HEADS = OUTPUTS // HEAD
 E_LOW = HEAD // OUT_TILES
 AHEAD = 2
-VECTOR_RELU_TILES = (0, 1, 2)
+LAG = 0
+B_ACT1, B_GROUPED, B_QUANT, B_ACT2, B_D, B_W, B_O = 2, 2, 4, 3, 8, 6, 3
+B_XT, B_PM, B_TV = 2, 3, 3
+SCALAR_RELU_TILES = (1, 5, 7)
+PLAIN_PAIRS = ()
 STAT_CHUNK = 512
+VECTOR_BLOCKS = 3
 
+ABS_SCALE = 0.5 if PLAIN_PAIRS else 1.0
 BN_EPS = 1e-5
 L1_EPS = 1e-12
 SELU_ALPHA = 1.6732632423543772
@@ -48,31 +54,31 @@ def tile_basicemotionpredictions_pa_t_e_kernel(tc, h2, gamma, beta, Wh_words, Wh
 
     with ExitStack() as ctx:
         const = ctx.enter_context(tc.tile_pool(name="const", bufs=1))
-        xpool = ctx.enter_context(tc.tile_pool(name="x", bufs=1))
-        act1 = ctx.enter_context(tc.tile_pool(name="act1", bufs=2))
-        quant = ctx.enter_context(tc.tile_pool(name="quant", bufs=4))
-        act2 = ctx.enter_context(tc.tile_pool(name="act2", bufs=3))
-        dpool = ctx.enter_context(tc.tile_pool(name="d", bufs=OUT_TILES))
-        wpool = ctx.enter_context(tc.tile_pool(name="w", bufs=6))
-        opool = ctx.enter_context(tc.tile_pool(name="o", bufs=3))
+        xpool = ctx.enter_context(tc.tile_pool(name="x", bufs=PASSES * N_BLOCKS))
+        act1 = ctx.enter_context(tc.tile_pool(name="act1", bufs=B_ACT1))
+        gpool = ctx.enter_context(tc.tile_pool(name="g", bufs=B_GROUPED))
+        quant = ctx.enter_context(tc.tile_pool(name="quant", bufs=B_QUANT))
+        act2 = ctx.enter_context(tc.tile_pool(name="act2", bufs=B_ACT2))
+        dpool = ctx.enter_context(tc.tile_pool(name="d", bufs=B_D))
+        wpool = ctx.enter_context(tc.tile_pool(name="w", bufs=B_W))
+        opool = ctx.enter_context(tc.tile_pool(name="o", bufs=B_O))
         small = ctx.enter_context(tc.tile_pool(name="small", bufs=2))
         scrap = ctx.enter_context(tc.tile_pool(name="scrap", bufs=4))
-        xt_psum = ctx.enter_context(tc.psum_pool(name="xt_psum", bufs=2))
-        pm_psum = ctx.enter_context(tc.psum_pool(name="pm_psum", bufs=3))
-        tv_psum = ctx.enter_context(tc.psum_pool(name="tv_psum", bufs=3))
+        xt_psum = ctx.enter_context(tc.psum_pool(name="xt_psum", bufs=B_XT))
+        pm_psum = ctx.enter_context(tc.psum_pool(name="pm_psum", bufs=B_PM))
+        tv_psum = ctx.enter_context(tc.psum_pool(name="tv_psum", bufs=B_TV))
 
-        x_blocks = []
-
-        def load_x(blk):
-            x_blk = xpool.tile([P, SUBS, FEATURES], BF16, name="x%d" % blk)
-            nc.sync.dma_start(
-                out=x_blk[:],
-                in_=h2[blk * BLOCK : (blk + 1) * BLOCK, :].rearrange("(p s) k -> p s k", s=SUBS),
-            )
-            x_blocks.append(x_blk)
-
-        for blk in range(N_BLOCKS):
-            load_x(blk)
+        x_tiles = {}
+        for c in range(PASSES):
+            for blk in range(N_BLOCKS):
+                x_tile = xpool.tile([P, SUBS, K_PASS], BF16, name="x_tile")
+                nc.sync.dma_start(
+                    out=x_tile[:],
+                    in_=h2[blk * BLOCK : (blk + 1) * BLOCK, c * K_PASS : (c + 1) * K_PASS].rearrange(
+                        "(p s) k -> p s k", s=SUBS
+                    ),
+                )
+                x_tiles[(blk, c)] = x_tile
 
         gamma_bf = const.tile([P, PASSES, PACK], BF16)
         beta_bf = const.tile([P, PASSES, PACK], BF16)
@@ -87,15 +93,18 @@ def tile_basicemotionpredictions_pa_t_e_kernel(tc, h2, gamma, beta, Wh_words, Wh
         ident = const.tile([P, P], F32)
         make_identity(nc, ident[:])
 
-        w_raw = act1.tile([P, PASSES, OUTPUTS], I32, name="w_raw", tag="lin")
-        planes_raw = act1.tile([P, PASSES, OUTPUTS // 4], I32, name="planes_raw", tag="neg")
+        w_raw = []
+        for c in range(PASSES):
+            w_pass = dpool.tile([P, OUTPUTS], I32, name="w_pass", tag="d_pair")
+            w_raw.append(w_pass)
+        planes_raw = wpool.tile([P, PASSES, OUTPUTS // 4], I32, name="planes_raw", tag="w_pair")
         w_words = const.tile([P, PASSES, OUTPUTS], U32, align_bytes=64)
         w_planes = const.tile([P, PASSES, OUTPUTS], U8, align_bytes=64)
         nc.vector.memset(planes_raw[:].rearrange("p c n -> p (c n)"), 0)
         words_dram = Wh_words.rearrange("g p n t -> g p (n t)").bitcast(I32).rearrange("(m c) p n -> c p m n", c=PASSES)
         scales_dram = Wh_scales.bitcast(I32).rearrange("(m c) q w -> c q m w", c=PASSES)
         for c in range(PASSES):
-            nc.sync.dma_start(out=w_raw[:, c, :].rearrange("p (m n) -> p m n", n=HEAD), in_=words_dram[c])
+            nc.sync.dma_start(out=w_raw[c][:].rearrange("p (m n) -> p m n", n=HEAD), in_=words_dram[c])
         for c in range(PASSES):
             for quad in range(4):
                 nc.sync.dma_start(
@@ -105,7 +114,7 @@ def tile_basicemotionpredictions_pa_t_e_kernel(tc, h2, gamma, beta, Wh_words, Wh
         for c in range(PASSES):
             nc.gpsimd.tensor_copy(
                 out=w_words[:, c, :].bitcast(I32).rearrange("p (j m e) -> p j m e", j=OUT_TILES, e=E_LOW),
-                in_=w_raw[:, c, :].rearrange("p (m j e) -> p j m e", j=OUT_TILES, e=E_LOW),
+                in_=w_raw[c][:].rearrange("p (m j e) -> p j m e", j=OUT_TILES, e=E_LOW),
             )
             nc.gpsimd.tensor_copy(
                 out=w_planes[:, c, :].bitcast(I32).rearrange("p (j m) -> p j m", j=OUT_TILES),
@@ -113,96 +122,117 @@ def tile_basicemotionpredictions_pa_t_e_kernel(tc, h2, gamma, beta, Wh_words, Wh
             )
 
         warm_in = const.tile([P, 1], F32)
-        warm_sqrt = const.tile([P, 1], F32)
         warm_exp = const.tile([P, 1], F32)
         nc.vector.memset(warm_in[:], 1.0)
-        nc.scalar.activation(out=warm_sqrt[:], in_=warm_in[:], func=ACT.Sqrt)
+        nc.scalar.activation(out=warm_exp[:], in_=warm_in[:], func=ACT.Exp)
 
         def transpose_features(blk, c, u, pool, tag):
-            x_words = x_blocks[blk][:].bitcast(F32)
+            x_words = x_tiles[(blk, c)][:].bitcast(F32)
             xt = pool.tile([P, BLOCK], F32, name="xt", tag=tag)
             for s in range(SUBS):
                 nc.tensor.transpose(
                     out=xt[:, s * P : (s + 1) * P],
-                    in_=x_words[:, s, 256 * c + u : 256 * (c + 1) : 2],
+                    in_=x_words[:, s, u : K_PASS // 2 : 2],
                     identity=ident[:],
                 )
             return xt
 
-        chunks = N_BLOCKS * 2 * BLOCK // STAT_CHUNK
-        vector_banks = 2 * PASSES - 1
-        n_feat = PASSES * PACK
-        stats = const.tile([P, vector_banks, chunks, 6], F32)
-        neg_pivot = const.tile([P, 2], F32)
-        sums = const.tile([P, 2, 2, N_BLOCKS], F32)
-        for blk in range(N_BLOCKS):
-            for c in range(PASSES):
+        zero = const.tile([P, 1], F32)
+        exp1_bias = const.tile([P, 1], F32)
+        minus_half = const.tile([P, PACK], F32)
+        nc.vector.memset(zero[:], 0.0)
+        nc.vector.memset(minus_half[:], -0.5)
+        nc.vector.tensor_scalar_add(out=exp1_bias[:], in0=zero[:], scalar1=SELU_ALPHA + math.log(SCALE_ALPHA))
+        parts = BLOCK * 2 // STAT_CHUNK
+        scalar_blocks = N_BLOCKS - VECTOR_BLOCKS
+        vector_rows = float(VECTOR_BLOCKS * BLOCK)
+        lin_scales = []
+        lin_biases = []
+        for c in range(PASSES):
+            stats0 = const.tile([P, N_BLOCKS * parts, 6], F32, name="stats0_%d" % c)
+            stats1 = const.tile([P, VECTOR_BLOCKS * parts, 6], F32, name="stats1_%d" % c)
+            neg_pivot = const.tile([P, 2], F32, name="neg_pivot_%d" % c)
+            sums = const.tile([P, 2, 2, scalar_blocks + 1], F32, name="sums_%d" % c)
+            mean_var = const.tile([P, PACK, 2], F32, name="mean_var_%d" % c)
+            first_mean_var = const.tile([P, 2, 2], F32, name="first_mean_var_%d" % c)
+            offset = const.tile([P, 2], F32, name="offset_%d" % c)
+            square = const.tile([P, 2], F32, name="square_%d" % c)
+            second = const.tile([P, 2], F32, name="second_%d" % c)
+            for blk in range(N_BLOCKS):
                 for u in range(2):
-                    if 2 * c + u < vector_banks:
+                    on_vector = u == 0 or blk < VECTOR_BLOCKS
+                    if on_vector:
                         xt = transpose_features(blk, c, u, xt_psum, "xt")
                     else:
                         xt = transpose_features(blk, c, u, tv_psum, "values")
                     pairs = xt[:].bitcast(BF16)
-                    if 2 * c + u < vector_banks:
-                        for h in range(2):
+                    if u == 1 and blk == 0:
+                        nc.vector.tensor_scalar_mul(out=neg_pivot[:], in0=pairs[:, 0:2], scalar1=-1.0)
+                    if on_vector:
+                        stats = stats1 if u else stats0
+                        for h in range(parts):
                             nc.vector.bn_stats(
-                                out=stats[:, 2 * c + u, 2 * blk + h, :],
-                                in_=pairs[:, h * STAT_CHUNK : (h + 1) * STAT_CHUNK],
+                                out=stats[:, parts * blk + h, :], in_=pairs[:, h * STAT_CHUNK : (h + 1) * STAT_CHUNK],
                             )
                     else:
-                        if blk == 0:
-                            nc.vector.tensor_scalar_mul(out=neg_pivot[:], in0=pairs[:, 0:2], scalar1=-1.0)
                         by_feature = pairs.rearrange("p (b e) -> p b e", e=2)
                         for e in range(2):
+                            column = blk - VECTOR_BLOCKS
                             centred = scrap.tile([P, BLOCK], BF16, name="centred")
                             squared = scrap.tile([P, BLOCK], BF16, name="squared")
                             nc.scalar.activation(
                                 out=centred[:], in_=by_feature[:, :, e], func=ACT.Identity,
-                                bias=neg_pivot[:, e : e + 1], scale=1.0, accum_out=sums[:, e, 0, blk : blk + 1],
+                                bias=neg_pivot[:, e : e + 1], scale=1.0, accum_out=sums[:, e, 0, column : column + 1],
                             )
                             nc.scalar.activation(
                                 out=squared[:], in_=by_feature[:, :, e], func=ACT.Square,
-                                bias=neg_pivot[:, e : e + 1], scale=1.0, accum_out=sums[:, e, 1, blk : blk + 1],
+                                bias=neg_pivot[:, e : e + 1], scale=1.0, accum_out=sums[:, e, 1, column : column + 1],
                             )
-        mean_var = const.tile([P, n_feat, 2], F32)
-        for cu in range(vector_banks):
+                    if u == 1 and blk == VECTOR_BLOCKS:
+                        for e in range(2):
+                            nc.vector.bn_aggr(out=first_mean_var[:, e, :], in_=stats1[:, :, 3 * e : 3 * e + 3])
+                        nc.vector.tensor_add(out=offset[:], in0=first_mean_var[:, :, 0], in1=neg_pivot[:])
+                        nc.vector.tensor_mul(out=square[:], in0=offset[:], in1=offset[:])
+                        nc.vector.tensor_add(out=second[:], in0=square[:], in1=first_mean_var[:, :, 1])
+                        nc.vector.tensor_scalar_mul(out=sums[:, :, 0, scalar_blocks], in0=offset[:], scalar1=vector_rows)
+                        nc.vector.tensor_scalar_mul(out=sums[:, :, 1, scalar_blocks], in0=second[:], scalar1=vector_rows)
             for e in range(2):
-                nc.vector.bn_aggr(out=mean_var[:, 2 * cu + e, :], in_=stats[:, cu, :, 3 * e : 3 * e + 3])
-        moments = const.tile([P, 2, 2], F32)
-        m1_squared = const.tile([P, 2], F32)
-        nc.vector.tensor_reduce(out=moments[:], in_=sums[:], axis=AXIS.X, op=ALU.add)
-        nc.vector.tensor_scalar_mul(out=moments[:], in0=moments[:], scalar1=1.0 / ROWS)
-        nc.vector.tensor_sub(out=mean_var[:, 2 * vector_banks :, 0], in0=moments[:, :, 0], in1=neg_pivot[:])
-        nc.vector.tensor_mul(out=m1_squared[:], in0=moments[:, :, 0], in1=moments[:, :, 0])
-        nc.vector.tensor_sub(out=mean_var[:, 2 * vector_banks :, 1], in0=moments[:, :, 1], in1=m1_squared[:])
+                nc.vector.bn_aggr(out=mean_var[:, e, :], in_=stats0[:, :, 3 * e : 3 * e + 3])
+            totals = const.tile([P, 2, 2], F32, name="totals_%d" % c)
+            moments = const.tile([P, 2, 2], F32, name="moments_%d" % c)
+            m1_squared = const.tile([P, 2], F32, name="m1_squared_%d" % c)
+            nc.vector.tensor_reduce(out=totals[:], in_=sums[:], axis=AXIS.X, op=ALU.add)
+            nc.vector.tensor_scalar_mul(out=moments[:], in0=totals[:], scalar1=1.0 / ROWS)
+            nc.vector.tensor_mul(out=m1_squared[:], in0=moments[:, :, 0], in1=moments[:, :, 0])
+            nc.vector.tensor_sub(out=mean_var[:, 2:, 0], in0=moments[:, :, 0], in1=neg_pivot[:])
+            nc.vector.tensor_sub(out=mean_var[:, 2:, 1], in0=moments[:, :, 1], in1=m1_squared[:])
 
-        var_eps = const.tile([P, n_feat], F32)
-        std = const.tile([P, n_feat], F32)
-        rstd = const.tile([P, n_feat], F32)
-        gain = const.tile([P, n_feat], F32)
-        mean_gain = const.tile([P, n_feat], F32)
-        shift = const.tile([P, n_feat], F32)
-        lin_scale = const.tile([P, n_feat], F32)
-        lin_bias = const.tile([P, n_feat], F32)
-        zero = const.tile([P, 1], F32)
-        exp1_bias = const.tile([P, 1], F32)
-        nc.vector.tensor_scalar_add(out=var_eps[:], in0=mean_var[:, :, 1], scalar1=BN_EPS)
-        nc.scalar.activation(out=std[:], in_=var_eps[:], func=ACT.Sqrt)
-        nc.scalar.activation(out=warm_exp[:], in_=std[:, 0:1], func=ACT.Exp)
-        nc.vector.reciprocal(out=rstd[:], in_=std[:])
-        nc.vector.tensor_mul(out=gain[:], in0=rstd[:], in1=gamma_bf[:].rearrange("p c t -> p (c t)"))
-        nc.vector.tensor_mul(out=mean_gain[:], in0=mean_var[:, :, 0], in1=gain[:])
-        nc.vector.tensor_sub(out=shift[:], in0=beta_bf[:].rearrange("p c t -> p (c t)"), in1=mean_gain[:])
-        nc.vector.tensor_scalar_mul(out=lin_scale[:], in0=gain[:], scalar1=SELU_SCALE)
-        nc.vector.tensor_scalar(
-            out=lin_bias[:], in0=shift[:], scalar1=SELU_SCALE, scalar2=-SCALE_ALPHA, op0=ALU.mult, op1=ALU.add,
-        )
-        nc.vector.memset(zero[:], 0.0)
-        nc.vector.tensor_scalar_add(out=exp1_bias[:], in0=zero[:], scalar1=SELU_ALPHA + math.log(SCALE_ALPHA))
+            var_eps = const.tile([P, PACK], F32, name="var_eps_%d" % c)
+            rstd = const.tile([P, PACK], F32, name="rstd_%d" % c)
+            lin_scale = const.tile([P, PACK], F32, name="lin_scale_%d" % c)
+            mean_scale = const.tile([P, PACK], F32, name="mean_scale_%d" % c)
+            beta_bias = const.tile([P, PACK], F32, name="beta_bias_%d" % c)
+            lin_bias = const.tile([P, PACK], F32, name="lin_bias_%d" % c)
+            nc.vector.tensor_scalar(
+                out=beta_bias[:], in0=beta_bf[:, c, :], scalar1=SELU_SCALE, scalar2=-SCALE_ALPHA, op0=ALU.mult, op1=ALU.add,
+            )
+            nc.vector.tensor_scalar_add(out=var_eps[:], in0=mean_var[:, :, 1], scalar1=BN_EPS)
+            nc.gpsimd.tensor_tensor(out=rstd[:], in0=var_eps[:], in1=minus_half[:], op=ALU.pow)
+            nc.vector.scalar_tensor_tensor(
+                out=lin_scale[:], in0=rstd[:], scalar=SELU_SCALE, in1=gamma_bf[:, c, :], op0=ALU.mult, op1=ALU.mult,
+            )
+            nc.vector.tensor_mul(out=mean_scale[:], in0=mean_var[:, :, 0], in1=lin_scale[:])
+            nc.vector.tensor_sub(out=lin_bias[:], in0=beta_bias[:], in1=mean_scale[:])
+            lin_scales.append(lin_scale)
+            lin_biases.append(lin_bias)
 
         relu2_bias = const.tile([P, OUT_TILES], F32)
         exp2_bias = const.tile([P, OUT_TILES], F32)
+        neg_bias = const.tile([P, OUT_TILES], F32)
+        cap_bias = const.tile([P, OUT_TILES], F32)
         nc.vector.tensor_copy(out=relu2_bias[:], in_=bh_bf[:])
+        nc.vector.tensor_scalar_mul(out=neg_bias[:], in0=bh_bf[:], scalar1=-1.0)
+        nc.vector.tensor_scalar_add(out=cap_bias[:], in0=bh_bf[:], scalar1=-SELU_ALPHA)
         nc.vector.tensor_scalar_add(out=exp2_bias[:], in0=bh_bf[:], scalar1=math.log(SELU_ALPHA))
 
         branches = {}
@@ -217,21 +247,20 @@ def tile_basicemotionpredictions_pa_t_e_kernel(tc, h2, gamma, beta, Wh_words, Wh
 
         def linear_branch(blk, c, u):
             if u == 0:
-                lin = act1.tile([P, PACK, BLOCK], F32, name="lin")
+                lin = act1.tile([P, P, PACK, SUBS], F32, name="lin")
                 branches[(blk, c)] = lin
             lin = branches[(blk, c)]
             xt = transpose_features(blk, c, u, xt_psum, "xt")
-            pairs = xt[:].bitcast(BF16).rearrange("p (b e) -> p b e", e=2)
+            pairs = xt[:].bitcast(BF16).rearrange("p (s r e) -> p r s e", r=P, e=2)
             for e in range(2):
                 t = 2 * u + e
-                f = PACK * c + t
                 nc.scalar.activation(
-                    out=lin[:, t, :], in_=pairs[:, :, e], func=ACT.Identity,
-                    bias=lin_bias[:, f : f + 1], scale=lin_scale[:, f : f + 1],
+                    out=lin[:, :, t, :], in_=pairs[:, :, :, e], func=ACT.Identity,
+                    bias=lin_biases[c][:, t : t + 1], scale=lin_scales[c][:, t : t + 1],
                 )
 
         def clamp(blk, c):
-            neg = act1.tile([P, PACK, BLOCK], F32, name="neg")
+            neg = act1.tile([P, P, PACK, SUBS], F32, name="neg")
             nc.vector.tensor_scalar_min(out=neg[:], in0=branches[(blk, c)][:], scalar1=-SCALE_ALPHA)
             clamped[(blk, c)] = neg
 
@@ -243,13 +272,13 @@ def tile_basicemotionpredictions_pa_t_e_kernel(tc, h2, gamma, beta, Wh_words, Wh
             exps[(blk, c)] = expo
 
         def join_e(blk, c):
-            grouped = act1.tile([P, BLOCK, PACK], BF16, name="grouped", align_bytes=64)
+            grouped = gpool.tile([P, SUBS, P * PACK], BF16, name="grouped", align_bytes=64)
             joined[(blk, c)] = grouped
             nc.vector.scalar_tensor_tensor(
                 out=grouped[:],
-                in0=branches[(blk, c)][:].rearrange("p t b -> p b t"),
+                in0=branches[(blk, c)][:].rearrange("p r t s -> p s (r t)"),
                 scalar=-SCALE_ALPHA,
-                in1=exps[(blk, c)][:].rearrange("p t b -> p b t"),
+                in1=exps[(blk, c)][:].rearrange("p r t s -> p s (r t)"),
                 op0=ALU.max,
                 op1=ALU.add,
             )
@@ -261,7 +290,7 @@ def tile_basicemotionpredictions_pa_t_e_kernel(tc, h2, gamma, beta, Wh_words, Wh
             nc.vector.quantize_mx(
                 out=e_words[:].bitcast(FP8X4),
                 scales=e_plane[:],
-                in_=grouped[:].rearrange("p b t -> p (b t)"),
+                in_=grouped[:].rearrange("p s n -> p (s n)"),
             )
             e_mx[(blk, c)] = (e_words, e_plane)
 
@@ -285,19 +314,26 @@ def tile_basicemotionpredictions_pa_t_e_kernel(tc, h2, gamma, beta, Wh_words, Wh
                 pairs[(blk, j // 2)] = (d_pair, w_pair)
             d_pair, w_pair = pairs[(blk, j // 2)]
             exp2 = act2.tile([P, BLOCK], F32, name="exp2")
-            pos = act2.tile([P, BLOCK], F32, name="pos")
             nc.scalar.activation(out=exp2[:], in_=pm[:], func=ACT.Exp, bias=exp2_bias[:, j : j + 1], scale=1.0)
-            if j in VECTOR_RELU_TILES:
-                nc.vector.tensor_scalar(
-                    out=pos[:], in0=pm[:], scalar1=relu2_bias[:, j : j + 1], scalar2=0.0, op0=ALU.add, op1=ALU.max,
+            if j in SCALAR_RELU_TILES:
+                if j // 2 in PLAIN_PAIRS:
+                    pos = w_pair[:, j % 2, :]
+                else:
+                    pos_tile = act2.tile([P, BLOCK], F32, name="pos_tile")
+                    pos = pos_tile[:]
+                nc.scalar.activation(out=pos, in_=pm[:], func=ACT.Relu, bias=relu2_bias[:, j : j + 1], scale=1.0)
+                nc.vector.scalar_tensor_tensor(
+                    out=d_pair[:, j % 2, :], in0=exp2[:], scalar=-SELU_ALPHA, in1=pos, op0=ALU.add, op1=ALU.min,
                 )
             else:
-                nc.scalar.activation(out=pos[:], in_=pm[:], func=ACT.Relu, bias=relu2_bias[:, j : j + 1], scale=1.0)
-            nc.vector.scalar_tensor_tensor(
-                out=d_pair[:, j % 2, :], in0=exp2[:], scalar=-SELU_ALPHA, in1=pos[:], op0=ALU.add, op1=ALU.min,
-            )
-            if j % 2 == 1:
-                nc.scalar.activation(out=w_pair[:], in_=d_pair[:], func=ACT.Abs)
+                nc.vector.tensor_scalar(
+                    out=exp2[:], in0=exp2[:], scalar1=SELU_ALPHA, scalar2=cap_bias[:, j : j + 1], op0=ALU.min, op1=ALU.add,
+                )
+                nc.vector.scalar_tensor_tensor(
+                    out=d_pair[:, j % 2, :], in0=pm[:], scalar=neg_bias[:, j : j + 1], in1=exp2[:], op0=ALU.max, op1=ALU.add,
+                )
+            if j % 2 == 1 and j // 2 not in PLAIN_PAIRS:
+                nc.scalar.activation(out=w_pair[:], in_=d_pair[:], func=ACT.Abs, scale=ABS_SCALE)
 
         def turned(dest, blk, j, which, s, start, stop):
             nc.tensor.matmul(
@@ -311,20 +347,42 @@ def tile_basicemotionpredictions_pa_t_e_kernel(tc, h2, gamma, beta, Wh_words, Wh
 
         def norm_sums(blk, s):
             if s == 0:
-                sums2[blk] = tv_psum.tile([P, SUBS, P], F32, name="sum_w", tag="values")
+                sum_w = tv_psum.tile([P, SUBS, P], F32, name="sum_w", tag="values")
+                sums2[blk] = [sum_w]
+                if PLAIN_PAIRS:
+                    sum_d = tv_psum.tile([P, SUBS, P], F32, name="sum_d", tag="values")
+                    sums2[blk].append(sum_d)
             for j in range(OUT_TILES):
-                turned(sums2[blk][:, s, :], blk, j, 1, s, j == 0, j == OUT_TILES - 1)
+                turned(sums2[blk][0][:, s, :], blk, j, 1, s, j == 0, j == OUT_TILES - 1)
+            plain = [2 * pair + k for pair in PLAIN_PAIRS for k in range(2)]
+            for j in plain:
+                turned(sums2[blk][1][:, s, :], blk, j, 0, s, j == plain[0], j == plain[-1])
 
-        def norm_finish(blk):
-            l1 = small.tile([P, SUBS * HEADS], F32, name="l1")
+        def norm_finish(blk, s0, n):
+            if s0 == 0:
+                inv = small.tile([P, SUBS, HEADS], F32, name="inv")
+                invs[blk] = inv
+            inv = invs[blk]
+            parts = []
+            for i, bank in enumerate(sums2[blk]):
+                part = small.tile([P, SUBS * HEADS], F32, name="part%d" % i)
+                nc.vector.tensor_reduce(
+                    out=part[:, : n * HEADS], in_=bank[:, s0 : s0 + n, :].rearrange("p s (m e) -> p (s m) e", e=E_LOW),
+                    axis=AXIS.X, op=ALU.add,
+                )
+                parts.append(part)
+            l1 = parts[0]
+            if PLAIN_PAIRS:
+                l1 = small.tile([P, SUBS * HEADS], F32, name="l1")
+                nc.vector.scalar_tensor_tensor(
+                    out=l1[:, : n * HEADS], in0=parts[0][:, : n * HEADS], scalar=2.0, in1=parts[1][:, : n * HEADS],
+                    op0=ALU.mult, op1=ALU.subtract,
+                )
             l1_floor = small.tile([P, SUBS * HEADS], F32, name="l1_floor")
-            inv = small.tile([P, SUBS, HEADS], F32, name="inv")
-            nc.vector.tensor_reduce(
-                out=l1[:], in_=sums2[blk][:].rearrange("p s (m e) -> p (s m) e", e=E_LOW), axis=AXIS.X, op=ALU.add,
+            nc.vector.tensor_scalar_max(out=l1_floor[:, : n * HEADS], in0=l1[:, : n * HEADS], scalar1=L1_EPS / SELU_SCALE)
+            nc.vector.reciprocal(
+                out=inv[:, s0 : s0 + n, :].rearrange("p s m -> p (s m)"), in_=l1_floor[:, : n * HEADS]
             )
-            nc.vector.tensor_scalar_max(out=l1_floor[:], in0=l1[:], scalar1=L1_EPS / SELU_SCALE)
-            nc.vector.reciprocal(out=inv[:].rearrange("p s m -> p (s m)"), in_=l1_floor[:])
-            invs[blk] = inv
 
         def normalise_and_store(blk, s, half):
             rows = out_rows[blk * BLOCK : (blk + 1) * BLOCK, :].rearrange("(p s) n -> p s n", s=SUBS)
@@ -345,10 +403,10 @@ def tile_basicemotionpredictions_pa_t_e_kernel(tc, h2, gamma, beta, Wh_words, Wh
             if half == 1:
                 nc.sync.dma_start(out=rows[:, s, :], in_=o[:].rearrange("p m e -> p (m e)"))
 
-        for step in range(-OUT_TILES - AHEAD, OUT_TILES * (N_BLOCKS + 1)):
+        for step in range(-OUT_TILES - AHEAD, OUT_TILES * (N_BLOCKS + 1) + LAG):
             blk, j = divmod(step, OUT_TILES)
             nxt, je = divmod(step + OUT_TILES + AHEAD, OUT_TILES)
-            prev = blk - 1
+            prev, jp = divmod(step - OUT_TILES - LAG, OUT_TILES)
             qb, qe = divmod(step - 1 + OUT_TILES + AHEAD, OUT_TILES)
             if je % 4 < 2 and nxt < N_BLOCKS:
                 linear_branch(nxt, je // 4, je % 4)
@@ -362,10 +420,21 @@ def tile_basicemotionpredictions_pa_t_e_kernel(tc, h2, gamma, beta, Wh_words, Wh
                 quantise_e(qb, qe // 4)
             if je % 4 == 3 and nxt < N_BLOCKS:
                 join_e(nxt, je // 4)
-            if prev >= 0 and j < SUBS:
-                norm_sums(prev, j)
-            if prev >= 0 and j == SUBS - 1:
-                norm_finish(prev)
-            if prev >= 0 and j >= SUBS:
-                normalise_and_store(prev, j - SUBS, 0)
-                normalise_and_store(prev, j - SUBS, 1)
+            if prev == N_BLOCKS - 1:
+                if jp < SUBS:
+                    norm_sums(prev, jp)
+                    norm_finish(prev, jp, 1)
+                    if jp > 0:
+                        normalise_and_store(prev, jp - 1, 0)
+                        normalise_and_store(prev, jp - 1, 1)
+                elif jp == SUBS:
+                    normalise_and_store(prev, jp - 1, 0)
+                    normalise_and_store(prev, jp - 1, 1)
+            elif prev >= 0:
+                if jp < SUBS:
+                    norm_sums(prev, jp)
+                if jp == SUBS - 1:
+                    norm_finish(prev, 0, SUBS)
+                if jp >= SUBS:
+                    normalise_and_store(prev, jp - SUBS, 0)
+                    normalise_and_store(prev, jp - SUBS, 1)

@@ -275,10 +275,10 @@ def tile_basicemotionpredictions_pa_t_e_kernel(tc, h2, gamma, beta, Wh_words, Wh
             grouped = gpool.tile([P, SUBS, P * PACK], BF16, name="grouped", align_bytes=64)
             joined[(blk, c)] = grouped
             nc.vector.scalar_tensor_tensor(
-                out=grouped[:],
-                in0=branches[(blk, c)][:].rearrange("p r t s -> p s (r t)"),
+                out=grouped[:].rearrange("p s n -> p n s"),
+                in0=branches[(blk, c)][:].rearrange("p r t s -> p (r t) s"),
                 scalar=-SCALE_ALPHA,
-                in1=exps[(blk, c)][:].rearrange("p r t s -> p s (r t)"),
+                in1=exps[(blk, c)][:].rearrange("p r t s -> p (r t) s"),
                 op0=ALU.max,
                 op1=ALU.add,
             )

@@ -29,15 +29,17 @@ OUT_TILES = OUTPUTS // P
 HALF_TILES = OUT_TILES // 2
 HEADS = OUTPUTS // HEAD
 E_LOW = HEAD // OUT_TILES
-AHEAD = 2
+AHEAD = 4
 LAG = 0
-B_ACT1, B_GROUPED, B_QUANT, B_ACT2, B_D, B_W, B_O = 2, 2, 4, 3, 8, 6, 3
+DEFER = 0
+B_ACT1, B_GROUPED, B_QUANT, B_ACT2, B_D, B_W, B_O = 3, 2, 6, 3, 8, 5, 3
 B_XT, B_PM, B_TV = 2, 3, 3
 SCALAR_RELU_TILES = (1, 5, 7)
 PLAIN_PAIRS = ()
 STAT_CHUNK = 512
-VECTOR_BLOCKS = 3
+VECTOR_BLOCKS = (3, 3)
 
+PARTS = 2 if PLAIN_PAIRS else 1
 ABS_SCALE = 0.5 if PLAIN_PAIRS else 1.0
 BN_EPS = 1e-5
 L1_EPS = 1e-12
@@ -144,15 +146,17 @@ def tile_basicemotionpredictions_pa_t_e_kernel(tc, h2, gamma, beta, Wh_words, Wh
         nc.vector.memset(minus_half[:], -0.5)
         nc.vector.tensor_scalar_add(out=exp1_bias[:], in0=zero[:], scalar1=SELU_ALPHA + math.log(SCALE_ALPHA))
         parts = BLOCK * 2 // STAT_CHUNK
-        scalar_blocks = N_BLOCKS - VECTOR_BLOCKS
-        vector_rows = float(VECTOR_BLOCKS * BLOCK)
         lin_scales = []
         lin_biases = []
         for c in range(PASSES):
+            vector_blocks = VECTOR_BLOCKS[c]
+            scalar_blocks = N_BLOCKS - vector_blocks
+            vector_rows = float(vector_blocks * BLOCK)
             stats0 = const.tile([P, N_BLOCKS * parts, 6], F32, name="stats0_%d" % c)
-            stats1 = const.tile([P, VECTOR_BLOCKS * parts, 6], F32, name="stats1_%d" % c)
+            stats1 = const.tile([P, vector_blocks * parts, 6], F32, name="stats1_%d" % c)
             neg_pivot = const.tile([P, 2], F32, name="neg_pivot_%d" % c)
-            sums = const.tile([P, 2, 2, scalar_blocks + 1], F32, name="sums_%d" % c)
+            sums = const.tile([P, 2, 2, scalar_blocks], F32, name="sums_%d" % c)
+            first_sums = const.tile([P, 2, 2], F32, name="first_sums_%d" % c)
             mean_var = const.tile([P, PACK, 2], F32, name="mean_var_%d" % c)
             first_mean_var = const.tile([P, 2, 2], F32, name="first_mean_var_%d" % c)
             offset = const.tile([P, 2], F32, name="offset_%d" % c)
@@ -160,7 +164,7 @@ def tile_basicemotionpredictions_pa_t_e_kernel(tc, h2, gamma, beta, Wh_words, Wh
             second = const.tile([P, 2], F32, name="second_%d" % c)
             for blk in range(N_BLOCKS):
                 for u in range(2):
-                    on_vector = u == 0 or blk < VECTOR_BLOCKS
+                    on_vector = u == 0 or blk < vector_blocks
                     if on_vector:
                         xt = transpose_features(blk, c, u, xt_psum, "xt")
                     else:
@@ -177,7 +181,7 @@ def tile_basicemotionpredictions_pa_t_e_kernel(tc, h2, gamma, beta, Wh_words, Wh
                     else:
                         by_feature = pairs.rearrange("p (b e) -> p b e", e=2)
                         for e in range(2):
-                            column = blk - VECTOR_BLOCKS
+                            column = blk - vector_blocks
                             centred = scrap.tile([P, BLOCK], BF16, name="centred")
                             squared = scrap.tile([P, BLOCK], BF16, name="squared")
                             nc.scalar.activation(
@@ -188,20 +192,22 @@ def tile_basicemotionpredictions_pa_t_e_kernel(tc, h2, gamma, beta, Wh_words, Wh
                                 out=squared[:], in_=by_feature[:, :, e], func=ACT.Square,
                                 bias=neg_pivot[:, e : e + 1], scale=1.0, accum_out=sums[:, e, 1, column : column + 1],
                             )
-                    if u == 1 and blk == VECTOR_BLOCKS:
+                    if u == 1 and blk == vector_blocks:
                         for e in range(2):
                             nc.vector.bn_aggr(out=first_mean_var[:, e, :], in_=stats1[:, :, 3 * e : 3 * e + 3])
-                        nc.vector.tensor_add(out=offset[:], in0=first_mean_var[:, :, 0], in1=neg_pivot[:])
-                        nc.vector.tensor_mul(out=square[:], in0=offset[:], in1=offset[:])
-                        nc.vector.tensor_add(out=second[:], in0=square[:], in1=first_mean_var[:, :, 1])
-                        nc.vector.tensor_scalar_mul(out=sums[:, :, 0, scalar_blocks], in0=offset[:], scalar1=vector_rows)
-                        nc.vector.tensor_scalar_mul(out=sums[:, :, 1, scalar_blocks], in0=second[:], scalar1=vector_rows)
+                        nc.gpsimd.tensor_tensor(out=offset[:], in0=first_mean_var[:, :, 0], in1=neg_pivot[:], op=ALU.add)
+                        nc.gpsimd.tensor_tensor(out=square[:], in0=offset[:], in1=offset[:], op=ALU.mult)
+                        nc.gpsimd.tensor_tensor(out=second[:], in0=square[:], in1=first_mean_var[:, :, 1], op=ALU.add)
+                        nc.gpsimd.tensor_scalar(out=first_sums[:, :, 0], in0=offset[:], scalar1=vector_rows, scalar2=0.0, op0=ALU.mult, op1=ALU.add)
+                        nc.gpsimd.tensor_scalar(out=first_sums[:, :, 1], in0=second[:], scalar1=vector_rows, scalar2=0.0, op0=ALU.mult, op1=ALU.add)
             for e in range(2):
                 nc.vector.bn_aggr(out=mean_var[:, e, :], in_=stats0[:, :, 3 * e : 3 * e + 3])
             totals = const.tile([P, 2, 2], F32, name="totals_%d" % c)
             moments = const.tile([P, 2, 2], F32, name="moments_%d" % c)
             m1_squared = const.tile([P, 2], F32, name="m1_squared_%d" % c)
-            nc.vector.tensor_reduce(out=totals[:], in_=sums[:], axis=AXIS.X, op=ALU.add)
+            later_sums = const.tile([P, 2, 2], F32, name="later_sums_%d" % c)
+            nc.vector.tensor_reduce(out=later_sums[:], in_=sums[:], axis=AXIS.X, op=ALU.add)
+            nc.vector.tensor_add(out=totals[:], in0=later_sums[:], in1=first_sums[:])
             nc.vector.tensor_scalar_mul(out=moments[:], in0=totals[:], scalar1=1.0 / ROWS)
             nc.vector.tensor_mul(out=m1_squared[:], in0=moments[:, :, 0], in1=moments[:, :, 0])
             nc.vector.tensor_sub(out=mean_var[:, 2:, 0], in0=moments[:, :, 0], in1=neg_pivot[:])
@@ -213,7 +219,7 @@ def tile_basicemotionpredictions_pa_t_e_kernel(tc, h2, gamma, beta, Wh_words, Wh
             mean_scale = const.tile([P, PACK], F32, name="mean_scale_%d" % c)
             beta_bias = const.tile([P, PACK], F32, name="beta_bias_%d" % c)
             lin_bias = const.tile([P, PACK], F32, name="lin_bias_%d" % c)
-            nc.vector.tensor_scalar(
+            nc.gpsimd.tensor_scalar(
                 out=beta_bias[:], in0=beta_bf[:, c, :], scalar1=SELU_SCALE, scalar2=-SCALE_ALPHA, op0=ALU.mult, op1=ALU.add,
             )
             nc.vector.tensor_scalar_add(out=var_eps[:], in0=mean_var[:, :, 1], scalar1=BN_EPS)
@@ -241,6 +247,7 @@ def tile_basicemotionpredictions_pa_t_e_kernel(tc, h2, gamma, beta, Wh_words, Wh
         joined = {}
         e_mx = {}
         pairs = {}
+        halves = {}
         sums2 = {}
         invs = {}
         outs = {}
@@ -308,32 +315,35 @@ def tile_basicemotionpredictions_pa_t_e_kernel(tc, h2, gamma, beta, Wh_words, Wh
                     start=(c == 0),
                     stop=(c == PASSES - 1),
                 )
+            exp2 = act2.tile([P, BLOCK], F32, name="exp2")
+            nc.scalar.activation(out=exp2[:], in_=pm[:], func=ACT.Exp, bias=exp2_bias[:, j : j + 1], scale=1.0)
+            if j in SCALAR_RELU_TILES:
+                pos = act2.tile([P, BLOCK], F32, name="pos")
+                nc.scalar.activation(out=pos[:], in_=pm[:], func=ACT.Relu, bias=relu2_bias[:, j : j + 1], scale=1.0)
+                halves[(blk, j)] = (exp2, pos)
+            else:
+                nc.vector.tensor_scalar(
+                    out=exp2[:], in0=exp2[:], scalar1=SELU_ALPHA, scalar2=cap_bias[:, j : j + 1], op0=ALU.min, op1=ALU.add,
+                )
+                halves[(blk, j)] = (exp2, pm)
+
+        def join_d(blk, j):
             if j % 2 == 0:
                 d_pair = dpool.tile([P, 2, BLOCK], F32, name="d_pair")
                 w_pair = wpool.tile([P, 2, BLOCK], F32, name="w_pair")
                 pairs[(blk, j // 2)] = (d_pair, w_pair)
             d_pair, w_pair = pairs[(blk, j // 2)]
-            exp2 = act2.tile([P, BLOCK], F32, name="exp2")
-            nc.scalar.activation(out=exp2[:], in_=pm[:], func=ACT.Exp, bias=exp2_bias[:, j : j + 1], scale=1.0)
+            exp2, other = halves[(blk, j)]
             if j in SCALAR_RELU_TILES:
-                if j // 2 in PLAIN_PAIRS:
-                    pos = w_pair[:, j % 2, :]
-                else:
-                    pos_tile = act2.tile([P, BLOCK], F32, name="pos_tile")
-                    pos = pos_tile[:]
-                nc.scalar.activation(out=pos, in_=pm[:], func=ACT.Relu, bias=relu2_bias[:, j : j + 1], scale=1.0)
                 nc.vector.scalar_tensor_tensor(
-                    out=d_pair[:, j % 2, :], in0=exp2[:], scalar=-SELU_ALPHA, in1=pos, op0=ALU.add, op1=ALU.min,
+                    out=d_pair[:, j % 2, :], in0=exp2[:], scalar=-SELU_ALPHA, in1=other[:], op0=ALU.add, op1=ALU.min,
                 )
             else:
-                nc.vector.tensor_scalar(
-                    out=exp2[:], in0=exp2[:], scalar1=SELU_ALPHA, scalar2=cap_bias[:, j : j + 1], op0=ALU.min, op1=ALU.add,
-                )
                 nc.vector.scalar_tensor_tensor(
-                    out=d_pair[:, j % 2, :], in0=pm[:], scalar=neg_bias[:, j : j + 1], in1=exp2[:], op0=ALU.max, op1=ALU.add,
+                    out=d_pair[:, j % 2, :], in0=other[:], scalar=neg_bias[:, j : j + 1], in1=exp2[:], op0=ALU.max, op1=ALU.add,
                 )
-            if j % 2 == 1 and j // 2 not in PLAIN_PAIRS:
-                nc.scalar.activation(out=w_pair[:], in_=d_pair[:], func=ACT.Abs, scale=ABS_SCALE)
+            if j % 2 == 1:
+                nc.scalar.activation(out=w_pair[:], in_=d_pair[:], func=ACT.Abs)
 
         def turned(dest, blk, j, which, s, start, stop):
             nc.tensor.matmul(
@@ -346,43 +356,34 @@ def tile_basicemotionpredictions_pa_t_e_kernel(tc, h2, gamma, beta, Wh_words, Wh
             )
 
         def norm_sums(blk, s):
-            if s == 0:
-                sum_w = tv_psum.tile([P, SUBS, P], F32, name="sum_w", tag="values")
-                sums2[blk] = [sum_w]
-                if PLAIN_PAIRS:
-                    sum_d = tv_psum.tile([P, SUBS, P], F32, name="sum_d", tag="values")
-                    sums2[blk].append(sum_d)
+            if s % 2 == 0:
+                sums2[(blk, s // 2)] = tv_psum.tile([P, PARTS, 2, P], F32, name="sums", tag="values")
+            bank = sums2[(blk, s // 2)]
             for j in range(OUT_TILES):
-                turned(sums2[blk][0][:, s, :], blk, j, 1, s, j == 0, j == OUT_TILES - 1)
+                turned(bank[:, 0, s % 2, :], blk, j, 1, s, j == 0, j == OUT_TILES - 1)
             plain = [2 * pair + k for pair in PLAIN_PAIRS for k in range(2)]
             for j in plain:
-                turned(sums2[blk][1][:, s, :], blk, j, 0, s, j == plain[0], j == plain[-1])
+                turned(bank[:, 1, s % 2, :], blk, j, 0, s, j == plain[0], j == plain[-1])
 
-        def norm_finish(blk, s0, n):
-            if s0 == 0:
-                inv = small.tile([P, SUBS, HEADS], F32, name="inv")
-                invs[blk] = inv
-            inv = invs[blk]
-            parts = []
-            for i, bank in enumerate(sums2[blk]):
-                part = small.tile([P, SUBS * HEADS], F32, name="part%d" % i)
-                nc.vector.tensor_reduce(
-                    out=part[:, : n * HEADS], in_=bank[:, s0 : s0 + n, :].rearrange("p s (m e) -> p (s m) e", e=E_LOW),
-                    axis=AXIS.X, op=ALU.add,
-                )
-                parts.append(part)
-            l1 = parts[0]
-            if PLAIN_PAIRS:
-                l1 = small.tile([P, SUBS * HEADS], F32, name="l1")
-                nc.vector.scalar_tensor_tensor(
-                    out=l1[:, : n * HEADS], in0=parts[0][:, : n * HEADS], scalar=2.0, in1=parts[1][:, : n * HEADS],
-                    op0=ALU.mult, op1=ALU.subtract,
-                )
-            l1_floor = small.tile([P, SUBS * HEADS], F32, name="l1_floor")
-            nc.vector.tensor_scalar_max(out=l1_floor[:, : n * HEADS], in0=l1[:, : n * HEADS], scalar1=L1_EPS / SELU_SCALE)
-            nc.vector.reciprocal(
-                out=inv[:, s0 : s0 + n, :].rearrange("p s m -> p (s m)"), in_=l1_floor[:, : n * HEADS]
+        def norm_finish(blk, pair):
+            if pair == 0:
+                invs[blk] = small.tile([P, SUBS, HEADS], F32, name="inv", tag="inv")
+            inv = invs[blk][:, 2 * pair : 2 * pair + 2, :].rearrange("p s m -> p (s m)")
+            parts = small.tile([P, PARTS, 2 * HEADS], F32, name="parts")
+            l1_floor = small.tile([P, 2 * HEADS], F32, name="l1_floor")
+            nc.vector.tensor_reduce(
+                out=parts[:].rearrange("p w n -> p (w n)"),
+                in_=sums2[(blk, pair)][:].rearrange("p w s (m e) -> p (w s m) e", e=E_LOW), axis=AXIS.X, op=ALU.add,
             )
+            l1 = parts[:, 0, :]
+            if PLAIN_PAIRS:
+                l1_tile = small.tile([P, 2 * HEADS], F32, name="l1_tile")
+                nc.vector.scalar_tensor_tensor(
+                    out=l1_tile[:], in0=parts[:, 0, :], scalar=2.0, in1=parts[:, 1, :], op0=ALU.mult, op1=ALU.subtract,
+                )
+                l1 = l1_tile[:]
+            nc.vector.tensor_scalar_max(out=l1_floor[:], in0=l1, scalar1=L1_EPS / SELU_SCALE)
+            nc.vector.reciprocal(out=inv, in_=l1_floor[:])
 
         def normalise_and_store(blk, s, half):
             rows = out_rows[blk * BLOCK : (blk + 1) * BLOCK, :].rearrange("(p s) n -> p s n", s=SUBS)
@@ -420,21 +421,17 @@ def tile_basicemotionpredictions_pa_t_e_kernel(tc, h2, gamma, beta, Wh_words, Wh
                 quantise_e(qb, qe // 4)
             if je % 4 == 3 and nxt < N_BLOCKS:
                 join_e(nxt, je // 4)
-            if prev == N_BLOCKS - 1:
+            if prev >= 0:
                 if jp < SUBS:
                     norm_sums(prev, jp)
-                    norm_finish(prev, jp, 1)
-                    if jp > 0:
-                        normalise_and_store(prev, jp - 1, 0)
-                        normalise_and_store(prev, jp - 1, 1)
-                elif jp == SUBS:
-                    normalise_and_store(prev, jp - 1, 0)
-                    normalise_and_store(prev, jp - 1, 1)
-            elif prev >= 0:
-                if jp < SUBS:
-                    norm_sums(prev, jp)
-                if jp == SUBS - 1:
-                    norm_finish(prev, 0, SUBS)
+                    if jp % 2 == 1:
+                        norm_finish(prev, jp // 2)
                 if jp >= SUBS:
                     normalise_and_store(prev, jp - SUBS, 0)
                     normalise_and_store(prev, jp - SUBS, 1)
+            if DEFER == 0 and 0 <= blk < N_BLOCKS:
+                join_d(blk, j)
+            if DEFER == 1:
+                b1, j1 = divmod(step - 1, OUT_TILES)
+                if 0 <= b1 < N_BLOCKS:
+                    join_d(b1, j1)

@@ -23,6 +23,7 @@ PACK = 4
 K_PASS = P * PACK
 PASSES = FEATURES // K_PASS
 BLOCK = 512
+GROUP = 4
 SUBS = BLOCK // P
 N_BLOCKS = ROWS // BLOCK
 OUT_TILES = OUTPUTS // P
@@ -31,22 +32,20 @@ HEADS = OUTPUTS // HEAD
 E_LOW = HEAD // OUT_TILES
 AHEAD = 4
 LAG = 0
-DEFER = 0
-B_ACT1, B_GROUPED, B_QUANT, B_ACT2, B_D, B_W, B_O = 3, 2, 6, 3, 8, 5, 3
+ROW_TILES = ROWS // P
+B_ACT1, B_GROUPED, B_QUANT, B_ACT2, B_D, B_W, B_O = 3, 2, 5, 4, 8, 6, 3
 B_XT, B_PM, B_TV = 2, 3, 3
 SCALAR_RELU_TILES = (1, 5, 7)
-PLAIN_PAIRS = ()
 STAT_CHUNK = 512
-VECTOR_BLOCKS = (3, 3)
+VECTOR_SHARE = ((6, 7), (0, 1, 2))
 
-PARTS = 2 if PLAIN_PAIRS else 1
-ABS_SCALE = 0.5 if PLAIN_PAIRS else 1.0
 BN_EPS = 1e-5
 L1_EPS = 1e-12
 SELU_ALPHA = 1.6732632423543772
 SELU_SCALE = 1.0507009873554805
 SCALE_ALPHA = SELU_SCALE * SELU_ALPHA
 
+RELUS = ((), (3, 7), (1, 3, 5, 7), (1, 3, 5, 7), (1, 3, 5, 7), (1, 3, 5, 7), (1, 2, 3, 5, 6, 7), (0, 1, 2, 3, 4, 5, 6, 7))
 FLOPS = 2 * ROWS * FEATURES * OUTPUTS
 
 
@@ -77,7 +76,7 @@ def tile_basicemotionpredictions_pa_t_e_kernel(tc, h2, gamma, beta, Wh_words, Wh
                 nc.sync.dma_start(
                     out=x_tile[:],
                     in_=h2[blk * BLOCK : (blk + 1) * BLOCK, c * K_PASS : (c + 1) * K_PASS].rearrange(
-                        "(p s) k -> p s k", s=SUBS
+                        "(s p) k -> p s k", s=SUBS
                     ),
                 )
                 x_tiles[(blk, c)] = x_tile
@@ -128,13 +127,13 @@ def tile_basicemotionpredictions_pa_t_e_kernel(tc, h2, gamma, beta, Wh_words, Wh
         nc.vector.memset(warm_in[:], 1.0)
         nc.scalar.activation(out=warm_exp[:], in_=warm_in[:], func=ACT.Exp)
 
-        def transpose_features(blk, c, u, pool, tag):
-            x_words = x_tiles[(blk, c)][:].bitcast(F32)
-            xt = pool.tile([P, BLOCK], F32, name="xt", tag=tag)
-            for s in range(SUBS):
+        def transpose_features(tiles, c, u, pool, tag):
+            xt = pool.tile([P, len(tiles) * P], F32, name="xt", tag=tag)
+            for i, tile in enumerate(tiles):
+                x_words = x_tiles[(tile // SUBS, c)][:].bitcast(F32)
                 nc.tensor.transpose(
-                    out=xt[:, s * P : (s + 1) * P],
-                    in_=x_words[:, s, u : K_PASS // 2 : 2],
+                    out=xt[:, i * P : (i + 1) * P],
+                    in_=x_words[:, tile % SUBS, u : K_PASS // 2 : 2],
                     identity=ident[:],
                 )
             return xt
@@ -149,13 +148,13 @@ def tile_basicemotionpredictions_pa_t_e_kernel(tc, h2, gamma, beta, Wh_words, Wh
         lin_scales = []
         lin_biases = []
         for c in range(PASSES):
-            vector_blocks = VECTOR_BLOCKS[c]
-            scalar_blocks = N_BLOCKS - vector_blocks
-            vector_rows = float(vector_blocks * BLOCK)
+            share = VECTOR_SHARE[c]
+            vector_rows = float(len(share) * BLOCK)
+            others = [blk for blk in range(N_BLOCKS) if blk not in share]
             stats0 = const.tile([P, N_BLOCKS * parts, 6], F32, name="stats0_%d" % c)
-            stats1 = const.tile([P, vector_blocks * parts, 6], F32, name="stats1_%d" % c)
+            stats1 = const.tile([P, len(share) * parts, 6], F32, name="stats1_%d" % c)
             neg_pivot = const.tile([P, 2], F32, name="neg_pivot_%d" % c)
-            sums = const.tile([P, 2, 2, scalar_blocks], F32, name="sums_%d" % c)
+            sums = const.tile([P, 2, 2, len(others)], F32, name="sums_%d" % c)
             first_sums = const.tile([P, 2, 2], F32, name="first_sums_%d" % c)
             mean_var = const.tile([P, PACK, 2], F32, name="mean_var_%d" % c)
             first_mean_var = const.tile([P, 2, 2], F32, name="first_mean_var_%d" % c)
@@ -163,25 +162,26 @@ def tile_basicemotionpredictions_pa_t_e_kernel(tc, h2, gamma, beta, Wh_words, Wh
             square = const.tile([P, 2], F32, name="square_%d" % c)
             second = const.tile([P, 2], F32, name="second_%d" % c)
             for blk in range(N_BLOCKS):
-                for u in range(2):
-                    on_vector = u == 0 or blk < vector_blocks
+                for u in (1, 0):
+                    on_vector = u == 0 or blk in share
                     if on_vector:
-                        xt = transpose_features(blk, c, u, xt_psum, "xt")
+                        xt = transpose_features(range(blk * SUBS, (blk + 1) * SUBS), c, u, xt_psum, "xt")
                     else:
-                        xt = transpose_features(blk, c, u, tv_psum, "values")
+                        xt = transpose_features(range(blk * SUBS, (blk + 1) * SUBS), c, u, tv_psum, "values")
                     pairs = xt[:].bitcast(BF16)
                     if u == 1 and blk == 0:
                         nc.vector.tensor_scalar_mul(out=neg_pivot[:], in0=pairs[:, 0:2], scalar1=-1.0)
                     if on_vector:
                         stats = stats1 if u else stats0
+                        first = parts * (share.index(blk) if u else blk)
                         for h in range(parts):
                             nc.vector.bn_stats(
-                                out=stats[:, parts * blk + h, :], in_=pairs[:, h * STAT_CHUNK : (h + 1) * STAT_CHUNK],
+                                out=stats[:, first + h, :], in_=pairs[:, h * STAT_CHUNK : (h + 1) * STAT_CHUNK],
                             )
                     else:
                         by_feature = pairs.rearrange("p (b e) -> p b e", e=2)
                         for e in range(2):
-                            column = blk - vector_blocks
+                            column = others.index(blk)
                             centred = scrap.tile([P, BLOCK], BF16, name="centred")
                             squared = scrap.tile([P, BLOCK], BF16, name="squared")
                             nc.scalar.activation(
@@ -192,7 +192,7 @@ def tile_basicemotionpredictions_pa_t_e_kernel(tc, h2, gamma, beta, Wh_words, Wh
                                 out=squared[:], in_=by_feature[:, :, e], func=ACT.Square,
                                 bias=neg_pivot[:, e : e + 1], scale=1.0, accum_out=sums[:, e, 1, column : column + 1],
                             )
-                    if u == 1 and blk == vector_blocks:
+                    if u == 0 and blk == share[-1]:
                         for e in range(2):
                             nc.vector.bn_aggr(out=first_mean_var[:, e, :], in_=stats1[:, :, 3 * e : 3 * e + 3])
                         nc.gpsimd.tensor_tensor(out=offset[:], in0=first_mean_var[:, :, 0], in1=neg_pivot[:], op=ALU.add)
@@ -241,8 +241,9 @@ def tile_basicemotionpredictions_pa_t_e_kernel(tc, h2, gamma, beta, Wh_words, Wh
         nc.vector.tensor_scalar_add(out=cap_bias[:], in0=bh_bf[:], scalar1=-SELU_ALPHA)
         nc.vector.tensor_scalar_add(out=exp2_bias[:], in0=bh_bf[:], scalar1=math.log(SELU_ALPHA))
 
+        units = [range(SUBS * blk, SUBS * (blk + 1)) for blk in range(N_BLOCKS)]
+        n_units = len(units)
         branches = {}
-        clamped = {}
         exps = {}
         joined = {}
         e_mx = {}
@@ -252,60 +253,56 @@ def tile_basicemotionpredictions_pa_t_e_kernel(tc, h2, gamma, beta, Wh_words, Wh
         invs = {}
         outs = {}
 
-        def linear_branch(blk, c, u):
-            if u == 0:
-                lin = act1.tile([P, P, PACK, SUBS], F32, name="lin")
-                branches[(blk, c)] = lin
-            lin = branches[(blk, c)]
-            xt = transpose_features(blk, c, u, xt_psum, "xt")
-            pairs = xt[:].bitcast(BF16).rearrange("p (s r e) -> p r s e", r=P, e=2)
+        def linear_branch(unit, c, bank):
+            if bank == 0:
+                lin = act1.tile([P, P, PACK, GROUP], F32, name="lin")
+                branches[(unit, c)] = lin
+            lin = branches[(unit, c)]
+            xt = transpose_features(units[unit], c, bank, xt_psum, "xt")
+            words = xt[:].bitcast(BF16).rearrange("p (q i e) -> p q i e", i=GROUP, e=2)
             for e in range(2):
-                t = 2 * u + e
+                t = 2 * bank + e
                 nc.scalar.activation(
-                    out=lin[:, :, t, :], in_=pairs[:, :, :, e], func=ACT.Identity,
+                    out=lin[:, :, t, :], in_=words[:, :, :, e], func=ACT.Identity,
                     bias=lin_biases[c][:, t : t + 1], scale=lin_scales[c][:, t : t + 1],
                 )
 
-        def clamp(blk, c):
-            neg = act1.tile([P, P, PACK, SUBS], F32, name="neg")
-            nc.vector.tensor_scalar_min(out=neg[:], in0=branches[(blk, c)][:], scalar1=-SCALE_ALPHA)
-            clamped[(blk, c)] = neg
+        def clamp(unit, c):
+            neg = act1.tile([P, P, PACK, GROUP], F32, name="neg")
+            nc.vector.tensor_scalar_min(out=neg[:], in0=branches[(unit, c)][:], scalar1=-SCALE_ALPHA)
+            exps[(unit, c)] = neg
 
-        def exp_branch(blk, c):
-            expo = clamped[(blk, c)]
+        def exp_branch(unit, c):
+            expo = exps[(unit, c)]
             nc.scalar.activation(
                 out=expo[:], in_=expo[:], func=ACT.Exp, bias=exp1_bias[:, 0:1], scale=1.0 / SELU_SCALE,
             )
-            exps[(blk, c)] = expo
 
-        def join_e(blk, c):
-            grouped = gpool.tile([P, SUBS, P * PACK], BF16, name="grouped", align_bytes=64)
-            joined[(blk, c)] = grouped
+        def join_e(unit, c):
+            grouped = gpool.tile([P, GROUP, P * PACK], BF16, name="grouped", align_bytes=64)
+            joined[(unit, c)] = grouped
             nc.vector.scalar_tensor_tensor(
-                out=grouped[:].rearrange("p s n -> p n s"),
-                in0=branches[(blk, c)][:].rearrange("p r t s -> p (r t) s"),
+                out=grouped[:].rearrange("p i n -> p n i"),
+                in0=branches[(unit, c)][:].rearrange("p q t i -> p (q t) i"),
                 scalar=-SCALE_ALPHA,
-                in1=exps[(blk, c)][:].rearrange("p r t s -> p (r t) s"),
+                in1=exps[(unit, c)][:].rearrange("p q t i -> p (q t) i"),
                 op0=ALU.max,
                 op1=ALU.add,
             )
 
-        def quantise_e(blk, c):
-            grouped = joined[(blk, c)]
-            e_words = quant.tile([P, BLOCK], U32, name="e_words", align_bytes=64)
-            e_plane = quant.tile([P, BLOCK], U8, name="e_plane", align_bytes=64)
-            nc.vector.quantize_mx(
-                out=e_words[:].bitcast(FP8X4),
-                scales=e_plane[:],
-                in_=grouped[:].rearrange("p s n -> p (s n)"),
-            )
-            e_mx[(blk, c)] = (e_words, e_plane)
+        def quantise_e(unit, c):
+            width = len(units[unit]) * P
+            e_words = quant.tile([P, width], U32, name="e_words", align_bytes=64)
+            e_plane = quant.tile([P, width], U8, name="e_plane", align_bytes=64)
+            nc.vector.quantize_mx(out=e_words[:].bitcast(FP8X4), scales=e_plane[:], in_=joined[(unit, c)][:].rearrange("p i n -> p (i n)"))
+            e_mx[(unit, c)] = (e_words, e_plane)
 
-        def heads(blk, j):
+        def heads(unit, j):
             cols = slice(j * P, (j + 1) * P)
-            pm = pm_psum.tile([P, BLOCK], F32, name="pm")
+            width = len(units[unit]) * P
+            pm = pm_psum.tile([P, width], F32, name="pm")
             for c in range(PASSES):
-                e_words, e_plane = e_mx[(blk, c)]
+                e_words, e_plane = e_mx[(unit, c)]
                 nc.tensor.matmul_mx(
                     out=pm[:],
                     lhsT=w_words[:, c, cols].bitcast(FP8X4),
@@ -315,26 +312,27 @@ def tile_basicemotionpredictions_pa_t_e_kernel(tc, h2, gamma, beta, Wh_words, Wh
                     start=(c == 0),
                     stop=(c == PASSES - 1),
                 )
-            exp2 = act2.tile([P, BLOCK], F32, name="exp2")
+            exp2 = act2.tile([P, width], F32, name="exp2")
             nc.scalar.activation(out=exp2[:], in_=pm[:], func=ACT.Exp, bias=exp2_bias[:, j : j + 1], scale=1.0)
-            if j in SCALAR_RELU_TILES:
-                pos = act2.tile([P, BLOCK], F32, name="pos")
+            if j in scalar_relus(unit):
+                pos = act2.tile([P, width], F32, name="pos")
                 nc.scalar.activation(out=pos[:], in_=pm[:], func=ACT.Relu, bias=relu2_bias[:, j : j + 1], scale=1.0)
-                halves[(blk, j)] = (exp2, pos)
+                halves[(unit, j)] = (exp2, pos)
             else:
                 nc.vector.tensor_scalar(
                     out=exp2[:], in0=exp2[:], scalar1=SELU_ALPHA, scalar2=cap_bias[:, j : j + 1], op0=ALU.min, op1=ALU.add,
                 )
-                halves[(blk, j)] = (exp2, pm)
+                halves[(unit, j)] = (exp2, pm)
 
-        def join_d(blk, j):
+        def join_d(unit, j):
+            width = len(units[unit]) * P
             if j % 2 == 0:
-                d_pair = dpool.tile([P, 2, BLOCK], F32, name="d_pair")
-                w_pair = wpool.tile([P, 2, BLOCK], F32, name="w_pair")
-                pairs[(blk, j // 2)] = (d_pair, w_pair)
-            d_pair, w_pair = pairs[(blk, j // 2)]
-            exp2, other = halves[(blk, j)]
-            if j in SCALAR_RELU_TILES:
+                d_pair = dpool.tile([P, 2, width], F32, name="d_pair")
+                w_pair = wpool.tile([P, 2, width], F32, name="w_pair")
+                pairs[(unit, j // 2)] = (d_pair, w_pair)
+            d_pair, w_pair = pairs[(unit, j // 2)]
+            exp2, other = halves[(unit, j)]
+            if j in scalar_relus(unit):
                 nc.vector.scalar_tensor_tensor(
                     out=d_pair[:, j % 2, :], in0=exp2[:], scalar=-SELU_ALPHA, in1=other[:], op0=ALU.add, op1=ALU.min,
                 )
@@ -345,93 +343,84 @@ def tile_basicemotionpredictions_pa_t_e_kernel(tc, h2, gamma, beta, Wh_words, Wh
             if j % 2 == 1:
                 nc.scalar.activation(out=w_pair[:], in_=d_pair[:], func=ACT.Abs)
 
-        def turned(dest, blk, j, which, s, start, stop):
+        def scalar_relus(unit):
+            return RELUS[unit]
+
+        def turned(dest, unit, j, which, i, start, stop):
             nc.tensor.matmul(
                 out=dest,
-                lhsT=pairs[(blk, j // 2)][which][:, j % 2, s * P : (s + 1) * P],
+                lhsT=pairs[(unit, j // 2)][which][:, j % 2, i * P : (i + 1) * P],
                 rhs=ident[:],
                 is_transpose=True,
                 start=start,
                 stop=stop,
             )
 
-        def norm_sums(blk, s):
-            if s % 2 == 0:
-                sums2[(blk, s // 2)] = tv_psum.tile([P, PARTS, 2, P], F32, name="sums", tag="values")
-            bank = sums2[(blk, s // 2)]
+        def norm_sums(unit, i):
+            if i % 2 == 0:
+                sums2[(unit, i // 2)] = tv_psum.tile([P, 2, P], F32, name="sums", tag="values")
             for j in range(OUT_TILES):
-                turned(bank[:, 0, s % 2, :], blk, j, 1, s, j == 0, j == OUT_TILES - 1)
-            plain = [2 * pair + k for pair in PLAIN_PAIRS for k in range(2)]
-            for j in plain:
-                turned(bank[:, 1, s % 2, :], blk, j, 0, s, j == plain[0], j == plain[-1])
+                turned(sums2[(unit, i // 2)][:, i % 2, :], unit, j, 1, i, j == 0, j == OUT_TILES - 1)
 
-        def norm_finish(blk, pair):
+        def norm_finish(unit, pair):
             if pair == 0:
-                invs[blk] = small.tile([P, SUBS, HEADS], F32, name="inv", tag="inv")
-            inv = invs[blk][:, 2 * pair : 2 * pair + 2, :].rearrange("p s m -> p (s m)")
-            parts = small.tile([P, PARTS, 2 * HEADS], F32, name="parts")
+                invs[unit] = small.tile([P, len(units[unit]), HEADS], F32, name="inv", tag="inv")
+            l1 = small.tile([P, 2 * HEADS], F32, name="l1")
             l1_floor = small.tile([P, 2 * HEADS], F32, name="l1_floor")
             nc.vector.tensor_reduce(
-                out=parts[:].rearrange("p w n -> p (w n)"),
-                in_=sums2[(blk, pair)][:].rearrange("p w s (m e) -> p (w s m) e", e=E_LOW), axis=AXIS.X, op=ALU.add,
+                out=l1[:], in_=sums2[(unit, pair)][:].rearrange("p s (m e) -> p (s m) e", e=E_LOW), axis=AXIS.X, op=ALU.add,
             )
-            l1 = parts[:, 0, :]
-            if PLAIN_PAIRS:
-                l1_tile = small.tile([P, 2 * HEADS], F32, name="l1_tile")
-                nc.vector.scalar_tensor_tensor(
-                    out=l1_tile[:], in0=parts[:, 0, :], scalar=2.0, in1=parts[:, 1, :], op0=ALU.mult, op1=ALU.subtract,
-                )
-                l1 = l1_tile[:]
-            nc.vector.tensor_scalar_max(out=l1_floor[:], in0=l1, scalar1=L1_EPS / SELU_SCALE)
-            nc.vector.reciprocal(out=inv, in_=l1_floor[:])
+            nc.vector.tensor_scalar_max(out=l1_floor[:], in0=l1[:], scalar1=L1_EPS / SELU_SCALE)
+            nc.vector.reciprocal(
+                out=invs[unit][:, 2 * pair : 2 * pair + 2, :].rearrange("p s m -> p (s m)"), in_=l1_floor[:]
+            )
 
-        def normalise_and_store(blk, s, half):
+        def normalise_and_store(unit, i, half):
+            tile = units[unit][i]
+            blk, s = divmod(tile, SUBS)
             rows = out_rows[blk * BLOCK : (blk + 1) * BLOCK, :].rearrange("(p s) n -> p s n", s=SUBS)
             values = tv_psum.tile([P, HEADS, HALF_TILES * E_LOW], F32, name="values")
             for jj in range(HALF_TILES):
-                turned(values[:, :, jj * E_LOW : (jj + 1) * E_LOW], blk, half * HALF_TILES + jj, 0, s, True, True)
+                turned(values[:, :, jj * E_LOW : (jj + 1) * E_LOW], unit, half * HALF_TILES + jj, 0, i, True, True)
             if half == 0:
                 o = opool.tile([P, HEADS, HEAD], F32, name="o")
-                outs[(blk, s)] = o
-            o = outs[(blk, s)]
+                outs[tile] = o
+            o = outs[tile]
             span = HALF_TILES * E_LOW
             nc.vector.tensor_tensor(
                 out=o[:, :, half * span : (half + 1) * span],
                 in0=values[:],
-                in1=invs[blk][:, s, :].unsqueeze(2).to_broadcast([P, HEADS, span]),
+                in1=invs[unit][:, i, :].unsqueeze(2).to_broadcast([P, HEADS, span]),
                 op=ALU.mult,
             )
             if half == 1:
                 nc.sync.dma_start(out=rows[:, s, :], in_=o[:].rearrange("p m e -> p (m e)"))
 
-        for step in range(-OUT_TILES - AHEAD, OUT_TILES * (N_BLOCKS + 1) + LAG):
-            blk, j = divmod(step, OUT_TILES)
+        for step in range(-OUT_TILES - AHEAD, OUT_TILES * (n_units + 1) + LAG):
+            unit, j = divmod(step, OUT_TILES)
             nxt, je = divmod(step + OUT_TILES + AHEAD, OUT_TILES)
             prev, jp = divmod(step - OUT_TILES - LAG, OUT_TILES)
-            qb, qe = divmod(step - 1 + OUT_TILES + AHEAD, OUT_TILES)
-            if je % 4 < 2 and nxt < N_BLOCKS:
+            qu, qe = divmod(step - 1 + OUT_TILES + AHEAD, OUT_TILES)
+            if je % 4 < 2 and nxt < n_units:
                 linear_branch(nxt, je // 4, je % 4)
-            if je % 4 == 1 and nxt < N_BLOCKS:
+            if je % 4 == 1 and nxt < n_units:
                 clamp(nxt, je // 4)
-            if je % 4 == 2 and nxt < N_BLOCKS:
+            if je % 4 == 2 and nxt < n_units:
                 exp_branch(nxt, je // 4)
-            if 0 <= blk < N_BLOCKS:
-                heads(blk, j)
-            if qe % 4 == 3 and 0 <= qb < N_BLOCKS:
-                quantise_e(qb, qe // 4)
-            if je % 4 == 3 and nxt < N_BLOCKS:
+            if 0 <= unit < n_units:
+                heads(unit, j)
+            if qe % 4 == 3 and 0 <= qu < n_units:
+                quantise_e(qu, qe // 4)
+            if je % 4 == 3 and nxt < n_units:
                 join_e(nxt, je // 4)
-            if prev >= 0:
-                if jp < SUBS:
+            if 0 <= prev < n_units:
+                count = len(units[prev])
+                if jp < count:
                     norm_sums(prev, jp)
                     if jp % 2 == 1:
                         norm_finish(prev, jp // 2)
-                if jp >= SUBS:
+                if SUBS <= jp < SUBS + count:
                     normalise_and_store(prev, jp - SUBS, 0)
                     normalise_and_store(prev, jp - SUBS, 1)
-            if DEFER == 0 and 0 <= blk < N_BLOCKS:
-                join_d(blk, j)
-            if DEFER == 1:
-                b1, j1 = divmod(step - 1, OUT_TILES)
-                if 0 <= b1 < N_BLOCKS:
-                    join_d(b1, j1)
+            if 0 <= unit < n_units:
+                join_d(unit, j)

import math
from contextlib import ExitStack

import concourse.mybir as mybir
from concourse.masks import make_identity

F32 = mybir.dt.float32
BF16 = mybir.dt.bfloat16
I32 = mybir.dt.int32
U32 = mybir.dt.uint32
U8 = mybir.dt.uint8
FP8X4 = mybir.dt.float8_e4m3fn_x4
ACT = mybir.ActivationFunctionType
ALU = mybir.AluOpType
AXIS = mybir.AxisListType

P = 128
ROWS = 4096
FEATURES = 1024
OUTPUTS = 1024
HEAD = 32
PACK = 4
K_PASS = P * PACK
PASSES = FEATURES // K_PASS
BLOCK = 512
GROUP = 4
SUBS = BLOCK // P
N_BLOCKS = ROWS // BLOCK
OUT_TILES = OUTPUTS // P
HALF_TILES = OUT_TILES // 2
HEADS = OUTPUTS // HEAD
E_LOW = HEAD // OUT_TILES
AHEAD = 4
LAG = 0
ROW_TILES = ROWS // P
B_ACT1, B_GROUPED, B_QUANT, B_ACT2, B_D, B_W, B_O = 3, 2, 5, 4, 8, 6, 3
B_XT, B_PM, B_TV = 2, 3, 3
SCALAR_RELU_TILES = (1, 5, 7)
STAT_CHUNK = 512
VECTOR_SHARE = ((6, 7), (0, 1, 2))

BN_EPS = 1e-5
L1_EPS = 1e-12
SELU_ALPHA = 1.6732632423543772
SELU_SCALE = 1.0507009873554805
SCALE_ALPHA = SELU_SCALE * SELU_ALPHA

RELUS = ((), (3, 7), (1, 3, 5, 7), (1, 3, 5, 7), (1, 3, 5, 7), (1, 3, 5, 7), (1, 2, 3, 5, 6, 7), (0, 1, 2, 3, 4, 5, 6, 7))
FLOPS = 2 * ROWS * FEATURES * OUTPUTS


def tile_basicemotionpredictions_pa_t_e_kernel(tc, h2, gamma, beta, Wh_words, Wh_scales, bh, out):
    nc = tc.nc
    out_rows = out.rearrange("b h g e -> b (h g e)")

    with ExitStack() as ctx:
        const = ctx.enter_context(tc.tile_pool(name="const", bufs=1))
        xpool = ctx.enter_context(tc.tile_pool(name="x", bufs=PASSES * N_BLOCKS))
        act1 = ctx.enter_context(tc.tile_pool(name="act1", bufs=B_ACT1))
        gpool = ctx.enter_context(tc.tile_pool(name="g", bufs=B_GROUPED))
        quant = ctx.enter_context(tc.tile_pool(name="quant", bufs=B_QUANT))
        act2 = ctx.enter_context(tc.tile_pool(name="act2", bufs=B_ACT2))
        dpool = ctx.enter_context(tc.tile_pool(name="d", bufs=B_D))
        wpool = ctx.enter_context(tc.tile_pool(name="w", bufs=B_W))
        opool = ctx.enter_context(tc.tile_pool(name="o", bufs=B_O))
        small = ctx.enter_context(tc.tile_pool(name="small", bufs=2))
        scrap = ctx.enter_context(tc.tile_pool(name="scrap", bufs=4))
        xt_psum = ctx.enter_context(tc.psum_pool(name="xt_psum", bufs=B_XT))
        pm_psum = ctx.enter_context(tc.psum_pool(name="pm_psum", bufs=B_PM))
        tv_psum = ctx.enter_context(tc.psum_pool(name="tv_psum", bufs=B_TV))

        x_tiles = {}
        for c in range(PASSES):
            for blk in range(N_BLOCKS):
                x_tile = xpool.tile([P, SUBS, K_PASS], BF16, name="x_tile")
                nc.sync.dma_start(
                    out=x_tile[:],
                    in_=h2[blk * BLOCK : (blk + 1) * BLOCK, c * K_PASS : (c + 1) * K_PASS].rearrange(
                        "(s p) k -> p s k", s=SUBS
                    ),
                )
                x_tiles[(blk, c)] = x_tile

        gamma_bf = const.tile([P, PASSES, PACK], BF16)
        beta_bf = const.tile([P, PASSES, PACK], BF16)
        nc.scalar.dma_start(out=gamma_bf[:], in_=gamma.rearrange("(c p t) -> p c t", c=PASSES, t=PACK))
        nc.scalar.dma_start(out=beta_bf[:], in_=beta.rearrange("(c p t) -> p c t", c=PASSES, t=PACK))
        bh_bf = const.tile([P, OUT_TILES], BF16)
        bh_heads = bh.rearrange("h g e -> (h g) e")
        with nc.allow_non_contiguous_dma(reason="1,024 bias values, one to a partition and column"):
            for e in range(E_LOW):
                nc.scalar.dma_start(out=bh_bf[e:P:E_LOW, :], in_=bh_heads[:, e:HEAD:E_LOW])

        ident = const.tile([P, P], F32)
        make_identity(nc, ident[:])

        w_raw = []
        for c in range(PASSES):
            w_pass = dpool.tile([P, OUTPUTS], I32, name="w_pass", tag="d_pair")
            w_raw.append(w_pass)
        planes_raw = wpool.tile([P, PASSES, OUTPUTS // 4], I32, name="planes_raw", tag="w_pair")
        w_words = const.tile([P, PASSES, OUTPUTS], U32, align_bytes=64)
        w_planes = const.tile([P, PASSES, OUTPUTS], U8, align_bytes=64)
        nc.vector.memset(planes_raw[:].rearrange("p c n -> p (c n)"), 0)
        words_dram = Wh_words.rearrange("g p n t -> g p (n t)").bitcast(I32).rearrange("(m c) p n -> c p m n", c=PASSES)
        scales_dram = Wh_scales.bitcast(I32).rearrange("(m c) q w -> c q m w", c=PASSES)
        for c in range(PASSES):
            nc.sync.dma_start(out=w_raw[c][:].rearrange("p (m n) -> p m n", n=HEAD), in_=words_dram[c])
        for c in range(PASSES):
            for quad in range(4):
                nc.sync.dma_start(
                    out=planes_raw[32 * quad : 32 * quad + 4, c, :].rearrange("r (m w) -> r m w", w=HEAD // 4),
                    in_=scales_dram[c, 4 * quad : 4 * quad + 4],
                )
        for c in range(PASSES):
            nc.gpsimd.tensor_copy(
                out=w_words[:, c, :].bitcast(I32).rearrange("p (j m e) -> p j m e", j=OUT_TILES, e=E_LOW),
                in_=w_raw[c][:].rearrange("p (m j e) -> p j m e", j=OUT_TILES, e=E_LOW),
            )
            nc.gpsimd.tensor_copy(
                out=w_planes[:, c, :].bitcast(I32).rearrange("p (j m) -> p j m", j=OUT_TILES),
                in_=planes_raw[:, c, :].rearrange("p (m j) -> p j m", j=OUT_TILES),
            )

        warm_in = const.tile([P, 1], F32)
        warm_exp = const.tile([P, 1], F32)
        nc.vector.memset(warm_in[:], 1.0)
        nc.scalar.activation(out=warm_exp[:], in_=warm_in[:], func=ACT.Exp)

        def transpose_features(tiles, c, u, pool, tag):
            xt = pool.tile([P, len(tiles) * P], F32, name="xt", tag=tag)
            for i, tile in enumerate(tiles):
                x_words = x_tiles[(tile // SUBS, c)][:].bitcast(F32)
                nc.tensor.transpose(
                    out=xt[:, i * P : (i + 1) * P],
                    in_=x_words[:, tile % SUBS, u : K_PASS // 2 : 2],
                    identity=ident[:],
                )
            return xt

        zero = const.tile([P, 1], F32)
        exp1_bias = const.tile([P, 1], F32)
        minus_half = const.tile([P, PACK], F32)
        nc.vector.memset(zero[:], 0.0)
        nc.vector.memset(minus_half[:], -0.5)
        nc.vector.tensor_scalar_add(out=exp1_bias[:], in0=zero[:], scalar1=SELU_ALPHA + math.log(SCALE_ALPHA))
        parts = BLOCK * 2 // STAT_CHUNK
        lin_scales = []
        lin_biases = []
        for c in range(PASSES):
            share = VECTOR_SHARE[c]
            vector_rows = float(len(share) * BLOCK)
            others = [blk for blk in range(N_BLOCKS) if blk not in share]
            stats0 = const.tile([P, N_BLOCKS * parts, 6], F32, name="stats0_%d" % c)
            stats1 = const.tile([P, len(share) * parts, 6], F32, name="stats1_%d" % c)
            neg_pivot = const.tile([P, 2], F32, name="neg_pivot_%d" % c)
            sums = const.tile([P, 2, 2, len(others)], F32, name="sums_%d" % c)
            first_sums = const.tile([P, 2, 2], F32, name="first_sums_%d" % c)
            mean_var = const.tile([P, PACK, 2], F32, name="mean_var_%d" % c)
            first_mean_var = const.tile([P, 2, 2], F32, name="first_mean_var_%d" % c)
            offset = const.tile([P, 2], F32, name="offset_%d" % c)
            square = const.tile([P, 2], F32, name="square_%d" % c)
            second = const.tile([P, 2], F32, name="second_%d" % c)
            for blk in range(N_BLOCKS):
                for u in (1, 0):
                    on_vector = u == 0 or blk in share
                    if on_vector:
                        xt = transpose_features(range(blk * SUBS, (blk + 1) * SUBS), c, u, xt_psum, "xt")
                    else:
                        xt = transpose_features(range(blk * SUBS, (blk + 1) * SUBS), c, u, tv_psum, "values")
                    pairs = xt[:].bitcast(BF16)
                    if u == 1 and blk == 0:
                        nc.vector.tensor_scalar_mul(out=neg_pivot[:], in0=pairs[:, 0:2], scalar1=-1.0)
                    if on_vector:
                        stats = stats1 if u else stats0
                        first = parts * (share.index(blk) if u else blk)
                        for h in range(parts):
                            nc.vector.bn_stats(
                                out=stats[:, first + h, :], in_=pairs[:, h * STAT_CHUNK : (h + 1) * STAT_CHUNK],
                            )
                    else:
                        by_feature = pairs.rearrange("p (b e) -> p b e", e=2)
                        for e in range(2):
                            column = others.index(blk)
                            centred = scrap.tile([P, BLOCK], BF16, name="centred")
                            squared = scrap.tile([P, BLOCK], BF16, name="squared")
                            nc.scalar.activation(
                                out=centred[:], in_=by_feature[:, :, e], func=ACT.Identity,
                                bias=neg_pivot[:, e : e + 1], scale=1.0, accum_out=sums[:, e, 0, column : column + 1],
                            )
                            nc.scalar.activation(
                                out=squared[:], in_=by_feature[:, :, e], func=ACT.Square,
                                bias=neg_pivot[:, e : e + 1], scale=1.0, accum_out=sums[:, e, 1, column : column + 1],
                            )
                    if u == 0 and blk == share[-1]:
                        for e in range(2):
                            nc.vector.bn_aggr(out=first_mean_var[:, e, :], in_=stats1[:, :, 3 * e : 3 * e + 3])
                        nc.gpsimd.tensor_tensor(out=offset[:], in0=first_mean_var[:, :, 0], in1=neg_pivot[:], op=ALU.add)
                        nc.gpsimd.tensor_tensor(out=square[:], in0=offset[:], in1=offset[:], op=ALU.mult)
                        nc.gpsimd.tensor_tensor(out=second[:], in0=square[:], in1=first_mean_var[:, :, 1], op=ALU.add)
                        nc.gpsimd.tensor_scalar(out=first_sums[:, :, 0], in0=offset[:], scalar1=vector_rows, scalar2=0.0, op0=ALU.mult, op1=ALU.add)
                        nc.gpsimd.tensor_scalar(out=first_sums[:, :, 1], in0=second[:], scalar1=vector_rows, scalar2=0.0, op0=ALU.mult, op1=ALU.add)
            for e in range(2):
                nc.vector.bn_aggr(out=mean_var[:, e, :], in_=stats0[:, :, 3 * e : 3 * e + 3])
            totals = const.tile([P, 2, 2], F32, name="totals_%d" % c)
            moments = const.tile([P, 2, 2], F32, name="moments_%d" % c)
            m1_squared = const.tile([P, 2], F32, name="m1_squared_%d" % c)
            later_sums = const.tile([P, 2, 2], F32, name="later_sums_%d" % c)
            nc.vector.tensor_reduce(out=later_sums[:], in_=sums[:], axis=AXIS.X, op=ALU.add)
            nc.vector.tensor_add(out=totals[:], in0=later_sums[:], in1=first_sums[:])
            nc.vector.tensor_scalar_mul(out=moments[:], in0=totals[:], scalar1=1.0 / ROWS)
            nc.vector.tensor_mul(out=m1_squared[:], in0=moments[:, :, 0], in1=moments[:, :, 0])
            nc.vector.tensor_sub(out=mean_var[:, 2:, 0], in0=moments[:, :, 0], in1=neg_pivot[:])
            nc.vector.tensor_sub(out=mean_var[:, 2:, 1], in0=moments[:, :, 1], in1=m1_squared[:])

            var_eps = const.tile([P, PACK], F32, name="var_eps_%d" % c)
            rstd = const.tile([P, PACK], F32, name="rstd_%d" % c)
            lin_scale = const.tile([P, PACK], F32, name="lin_scale_%d" % c)
            mean_scale = const.tile([P, PACK], F32, name="mean_scale_%d" % c)
            beta_bias = const.tile([P, PACK], F32, name="beta_bias_%d" % c)
            lin_bias = const.tile([P, PACK], F32, name="lin_bias_%d" % c)
            nc.gpsimd.tensor_scalar(
                out=beta_bias[:], in0=beta_bf[:, c, :], scalar1=SELU_SCALE, scalar2=-SCALE_ALPHA, op0=ALU.mult, op1=ALU.add,
            )
            nc.vector.tensor_scalar_add(out=var_eps[:], in0=mean_var[:, :, 1], scalar1=BN_EPS)
            nc.gpsimd.tensor_tensor(out=rstd[:], in0=var_eps[:], in1=minus_half[:], op=ALU.pow)
            nc.vector.scalar_tensor_tensor(
                out=lin_scale[:], in0=rstd[:], scalar=SELU_SCALE, in1=gamma_bf[:, c, :], op0=ALU.mult, op1=ALU.mult,
            )
            nc.vector.tensor_mul(out=mean_scale[:], in0=mean_var[:, :, 0], in1=lin_scale[:])
            nc.vector.tensor_sub(out=lin_bias[:], in0=beta_bias[:], in1=mean_scale[:])
            lin_scales.append(lin_scale)
            lin_biases.append(lin_bias)

        relu2_bias = const.tile([P, OUT_TILES], F32)
        exp2_bias = const.tile([P, OUT_TILES], F32)
        neg_bias = const.tile([P, OUT_TILES], F32)
        cap_bias = const.tile([P, OUT_TILES], F32)
        nc.vector.tensor_copy(out=relu2_bias[:], in_=bh_bf[:])
        nc.vector.tensor_scalar_mul(out=neg_bias[:], in0=bh_bf[:], scalar1=-1.0)
        nc.vector.tensor_scalar_add(out=cap_bias[:], in0=bh_bf[:], scalar1=-SELU_ALPHA)
        nc.vector.tensor_scalar_add(out=exp2_bias[:], in0=bh_bf[:], scalar1=math.log(SELU_ALPHA))

        units = [range(SUBS * blk, SUBS * (blk + 1)) for blk in range(N_BLOCKS)]
        n_units = len(units)
        branches = {}
        exps = {}
        joined = {}
        e_mx = {}
        pairs = {}
        halves = {}
        sums2 = {}
        invs = {}
        outs = {}

        def linear_branch(unit, c, bank):
            if bank == 0:
                lin = act1.tile([P, P, PACK, GROUP], F32, name="lin")
                branches[(unit, c)] = lin
            lin = branches[(unit, c)]
            xt = transpose_features(units[unit], c, bank, xt_psum, "xt")
            words = xt[:].bitcast(BF16).rearrange("p (q i e) -> p q i e", i=GROUP, e=2)
            for e in range(2):
                t = 2 * bank + e
                nc.scalar.activation(
                    out=lin[:, :, t, :], in_=words[:, :, :, e], func=ACT.Identity,
                    bias=lin_biases[c][:, t : t + 1], scale=lin_scales[c][:, t : t + 1],
                )

        def clamp(unit, c):
            neg = act1.tile([P, P, PACK, GROUP], F32, name="neg")
            nc.vector.tensor_scalar_min(out=neg[:], in0=branches[(unit, c)][:], scalar1=-SCALE_ALPHA)
            exps[(unit, c)] = neg

        def exp_branch(unit, c):
            expo = exps[(unit, c)]
            nc.scalar.activation(
                out=expo[:], in_=expo[:], func=ACT.Exp, bias=exp1_bias[:, 0:1], scale=1.0 / SELU_SCALE,
            )

        def join_e(unit, c):
            grouped = gpool.tile([P, GROUP, P * PACK], BF16, name="grouped", align_bytes=64)
            joined[(unit, c)] = grouped
            nc.vector.scalar_tensor_tensor(
                out=grouped[:].rearrange("p i n -> p n i"),
                in0=branches[(unit, c)][:].rearrange("p q t i -> p (q t) i"),
                scalar=-SCALE_ALPHA,
                in1=exps[(unit, c)][:].rearrange("p q t i -> p (q t) i"),
                op0=ALU.max,
                op1=ALU.add,
            )

        def quantise_e(unit, c):
            width = len(units[unit]) * P
            e_words = quant.tile([P, width], U32, name="e_words", align_bytes=64)
            e_plane = quant.tile([P, width], U8, name="e_plane", align_bytes=64)
            nc.vector.quantize_mx(out=e_words[:].bitcast(FP8X4), scales=e_plane[:], in_=joined[(unit, c)][:].rearrange("p i n -> p (i n)"))
            e_mx[(unit, c)] = (e_words, e_plane)

        def heads(unit, j):
            cols = slice(j * P, (j + 1) * P)
            width = len(units[unit]) * P
            pm = pm_psum.tile([P, width], F32, name="pm")
            for c in range(PASSES):
                e_words, e_plane = e_mx[(unit, c)]
                nc.tensor.matmul_mx(
                    out=pm[:],
                    lhsT=w_words[:, c, cols].bitcast(FP8X4),
                    lhsT_scale=w_planes[:, c, cols],
                    rhs=e_words[:].bitcast(FP8X4),
                    rhs_scale=e_plane[:],
                    start=(c == 0),
                    stop=(c == PASSES - 1),
                )
            exp2 = act2.tile([P, width], F32, name="exp2")
            nc.scalar.activation(out=exp2[:], in_=pm[:], func=ACT.Exp, bias=exp2_bias[:, j : j + 1], scale=1.0)
            if j in scalar_relus(unit):
                pos = act2.tile([P, width], F32, name="pos")
                nc.scalar.activation(out=pos[:], in_=pm[:], func=ACT.Relu, bias=relu2_bias[:, j : j + 1], scale=1.0)
                halves[(unit, j)] = (exp2, pos)
            else:
                nc.vector.tensor_scalar(
                    out=exp2[:], in0=exp2[:], scalar1=SELU_ALPHA, scalar2=cap_bias[:, j : j + 1], op0=ALU.min, op1=ALU.add,
                )
                halves[(unit, j)] = (exp2, pm)

        def join_d(unit, j):
            width = len(units[unit]) * P
            if j % 2 == 0:
                d_pair = dpool.tile([P, 2, width], F32, name="d_pair")
                w_pair = wpool.tile([P, 2, width], F32, name="w_pair")
                pairs[(unit, j // 2)] = (d_pair, w_pair)
            d_pair, w_pair = pairs[(unit, j // 2)]
            exp2, other = halves[(unit, j)]
            if j in scalar_relus(unit):
                nc.vector.scalar_tensor_tensor(
                    out=d_pair[:, j % 2, :], in0=exp2[:], scalar=-SELU_ALPHA, in1=other[:], op0=ALU.add, op1=ALU.min,
                )
            else:
                nc.vector.scalar_tensor_tensor(
                    out=d_pair[:, j % 2, :], in0=other[:], scalar=neg_bias[:, j : j + 1], in1=exp2[:], op0=ALU.max, op1=ALU.add,
                )
            if j % 2 == 1:
                nc.scalar.activation(out=w_pair[:], in_=d_pair[:], func=ACT.Abs)

        def scalar_relus(unit):
            return RELUS[unit]

        def turned(dest, unit, j, which, i, start, stop):
            nc.tensor.matmul(
                out=dest,
                lhsT=pairs[(unit, j // 2)][which][:, j % 2, i * P : (i + 1) * P],
                rhs=ident[:],
                is_transpose=True,
                start=start,
                stop=stop,
            )

        def norm_sums(unit, i):
            if i % 2 == 0:
                sums2[(unit, i // 2)] = tv_psum.tile([P, 2, P], F32, name="sums", tag="values")
            for j in range(OUT_TILES):
                turned(sums2[(unit, i // 2)][:, i % 2, :], unit, j, 1, i, j == 0, j == OUT_TILES - 1)

        def norm_finish(unit, pair):
            if pair == 0:
                invs[unit] = small.tile([P, len(units[unit]), HEADS], F32, name="inv", tag="inv")
            l1 = small.tile([P, 2 * HEADS], F32, name="l1")
            l1_floor = small.tile([P, 2 * HEADS], F32, name="l1_floor")
            nc.vector.tensor_reduce(
                out=l1[:], in_=sums2[(unit, pair)][:].rearrange("p s (m e) -> p (s m) e", e=E_LOW), axis=AXIS.X, op=ALU.add,
            )
            nc.vector.tensor_scalar_max(out=l1_floor[:], in0=l1[:], scalar1=L1_EPS / SELU_SCALE)
            nc.vector.reciprocal(
                out=invs[unit][:, 2 * pair : 2 * pair + 2, :].rearrange("p s m -> p (s m)"), in_=l1_floor[:]
            )

        def normalise_and_store(unit, i, half):
            tile = units[unit][i]
            blk, s = divmod(tile, SUBS)
            rows = out_rows[blk * BLOCK : (blk + 1) * BLOCK, :].rearrange("(p s) n -> p s n", s=SUBS)
            values = tv_psum.tile([P, HEADS, HALF_TILES * E_LOW], F32, name="values")
            for jj in range(HALF_TILES):
                turned(values[:, :, jj * E_LOW : (jj + 1) * E_LOW], unit, half * HALF_TILES + jj, 0, i, True, True)
            if half == 0:
                o = opool.tile([P, HEADS, HEAD], F32, name="o")
                outs[tile] = o
            o = outs[tile]
            span = HALF_TILES * E_LOW
            nc.vector.tensor_tensor(
                out=o[:, :, half * span : (half + 1) * span],
                in0=values[:],
                in1=invs[unit][:, i, :].unsqueeze(2).to_broadcast([P, HEADS, span]),
                op=ALU.mult,
            )
            if half == 1:
                nc.sync.dma_start(out=rows[:, s, :], in_=o[:].rearrange("p m e -> p (m e)"))

        for step in range(-OUT_TILES - AHEAD, OUT_TILES * (n_units + 1) + LAG):
            unit, j = divmod(step, OUT_TILES)
            nxt, je = divmod(step + OUT_TILES + AHEAD, OUT_TILES)
            prev, jp = divmod(step - OUT_TILES - LAG, OUT_TILES)
            qu, qe = divmod(step - 1 + OUT_TILES + AHEAD, OUT_TILES)
            if je % 4 < 2 and nxt < n_units:
                linear_branch(nxt, je // 4, je % 4)
            if je % 4 == 1 and nxt < n_units:
                clamp(nxt, je // 4)
            if je % 4 == 2 and nxt < n_units:
                exp_branch(nxt, je // 4)
            if 0 <= unit < n_units:
                heads(unit, j)
            if qe % 4 == 3 and 0 <= qu < n_units:
                quantise_e(qu, qe // 4)
            if je % 4 == 3 and nxt < n_units:
                join_e(nxt, je // 4)
            if 0 <= prev < n_units:
                count = len(units[prev])
                if jp < count:
                    norm_sums(prev, jp)
                    if jp % 2 == 1:
                        norm_finish(prev, jp // 2)
                if SUBS <= jp < SUBS + count:
                    normalise_and_store(prev, jp - SUBS, 0)
                    normalise_and_store(prev, jp - SUBS, 1)
            if 0 <= unit < n_units:
                join_d(unit, j)
